import numpy as np
import ml_dtypes


def mxq(x, axis, fmt="e4m3"):
    dtype, down = {"e4m3": (ml_dtypes.float8_e4m3fn, 7), "e5m2": (ml_dtypes.float8_e5m2, 14)}[fmt]
    v = np.moveaxis(np.asarray(x, np.float32).astype(ml_dtypes.bfloat16).astype(np.float64), axis, -1)
    blocks = v.reshape(v.shape[:-1] + (-1, 32))
    amax = np.abs(blocks).max(-1, keepdims=True)
    byte = np.maximum(np.where(amax > 0, np.frexp(amax)[1] - 1 + 127, 0) - down, 1)
    scale = np.exp2(byte - 127.0)
    codes = (blocks / scale).astype(np.float32).astype(dtype).astype(np.float64)
    return np.moveaxis((codes * scale).reshape(v.shape), -1, axis)


WIDE = False


def mx_kscale(k):
    if not WIDE:
        return np.ones(k)
    levels = np.array([10, -10, 5, -5, 0])
    a = np.random.permutation(np.resize(levels, k // 512 * 4)).reshape(k // 512, 4)
    idx = np.arange(k)
    return np.exp2(a[idx // 512, idx % 128 // 32])


BF16 = ml_dtypes.bfloat16


def bf(x):
    return np.asarray(x, np.float32).astype(BF16)


def f64(x):
    return np.asarray(x).astype(np.float64)


B, S, E, H, DH = 1, 512, 1536, 12, 128
NEG = -10000.0


def setup_inputs():
    t = mx_kscale(E)
    return {"q_rot": bf(np.random.standard_normal((B, S, H, DH)) * 1.25),
            "k_rot": bf(np.random.standard_normal((B, S, H, DH)) * 1.25),
            "v": bf(np.abs(np.random.standard_normal((B, S, H, DH))) * 1.25 * t.reshape(H, DH)),
            "feat_mask": bf(1.0 + 0.25 * np.random.standard_normal(E)),
            "wo_w": bf(np.random.standard_normal((E, E)) * 1.5 / np.sqrt(E) / t[None, :]),
            "wo_b": bf(np.random.standard_normal(E) * 0.2)}


def reference(q_rot, k_rot, v, feat_mask, wo_w, wo_b):
    scores = (f64(q_rot).transpose(0, 2, 1, 3) @ f64(k_rot).transpose(0, 2, 3, 1)) * (1.0 / np.sqrt(DH))
    scores = scores + np.triu(np.full((S, S), NEG), 1)
    e = np.exp(scores - scores.max(-1, keepdims=True))
    ctx = (mxq(e, 3, "e4m3") @ mxq(f64(v).transpose(0, 2, 1, 3), 2, "e4m3")) / e.sum(-1, keepdims=True)
    ctx = ctx.transpose(0, 2, 1, 3).reshape(B, S, E)
    fm = f64(feat_mask)
    ctx = ctx * fm
    out = (mxq(ctx, 2, "e4m3") @ mxq(f64(wo_w), 1, "e4m3").T) + f64(wo_b)
    return out * fm

@@ -1,0 +1,332 @@
+import math
+from contextlib import ExitStack
+
+import concourse.mybir as mybir
+from concourse.masks import make_identity
+
+BF16 = mybir.dt.bfloat16
+F32 = mybir.dt.float32
+U32 = mybir.dt.uint32
+U8 = mybir.dt.uint8
+FP8X4 = mybir.dt.float8_e4m3fn_x4
+ALU = mybir.AluOpType
+ACT = mybir.ActivationFunctionType
+AXIS = mybir.AxisListType
+
+P = 128
+PACK = 4
+S = 512
+H = 12
+DH = 128
+E = H * DH
+BLOCKS = S // P
+GROUP = PACK
+GROUPS = H // GROUP
+CHUNK = 512
+CHUNKS = E // CHUNK
+SCALE = 1.0 / math.sqrt(DH)
+MASK_RAW = -10000.0 * math.sqrt(DH)
+
+FLOPS = 2 * H * S * S * DH * 2 + 2 * S * E * E
+
+
+W_PIECES = GROUPS * CHUNKS
+W_PER_ROUND = 2
+W_FIRST_ROUND = 3
+
+
+def tile_onedscaleparallelmha_pb_kernel(tc, q_rot, k_rot, v, feat_mask, wo_w, wo_b, out):
+    nc = tc.nc
+    steps = [(i, g) for i in range(BLOCKS) for g in range(GROUPS)]
+
+    with ExitStack() as stack:
+        const = stack.enter_context(tc.tile_pool(name="const", bufs=1))
+        keep = stack.enter_context(tc.tile_pool(name="keep", bufs=1))
+        work = stack.enter_context(tc.tile_pool(name="work", bufs=3))
+        small = stack.enter_context(tc.tile_pool(name="small", bufs=8))
+        ps_scores = stack.enter_context(tc.psum_pool(name="ps_scores", bufs=4))
+        ps_turn = stack.enter_context(tc.psum_pool(name="ps_turn", bufs=3))
+        ps_ctx = stack.enter_context(tc.psum_pool(name="ps_ctx", bufs=1))
+        stack.enter_context(tc.manual_schedule())
+
+        q_rows = q_rot.rearrange("b (i p) h d -> (b i) p (h d)", p=P)
+        k_rows = k_rot.rearrange("b (i p) h d -> (b i) p (h d)", p=P)
+        w_rows = wo_w.rearrange("(b p) f -> p b f", p=P)
+        q_sb = keep.tile([P, BLOCKS, E], BF16)
+        k_sb = keep.tile([P, BLOCKS, E], BF16)
+        v_sb = keep.tile([P, PACK, E], BF16)
+        w_sb = keep.tile([P, H, E], BF16)
+        fm_bc = const.tile([P, E], BF16)
+        b_bc = const.tile([P, E], BF16)
+        for i, g in steps:
+            cols = slice(g * GROUP * DH, (g + 1) * GROUP * DH)
+            nc.sync.dma_start(out=q_sb[:, i, cols], in_=q_rows[i][:, cols])
+            nc.sync.dma_start(out=k_sb[:, i, cols], in_=k_rows[i][:, cols])
+            if (i, g) == (0, GROUPS - 1):
+                nc.sync.dma_start(
+                    out=v_sb[:].rearrange("p (c e) f -> p c (e f)", c=2),
+                    in_=v.rearrange("b (c p e) h d -> p (b c) (e h d)", c=2, e=2),
+                )
+                nc.sync.dma_start(out=fm_bc[:], in_=feat_mask.partition_broadcast(P))
+        for c in range(CHUNKS):
+            nc.sync.dma_start(out=w_sb[:, 4 * c : 4 * c + 4, :], in_=w_rows[:, 4 * c : 4 * c + 4, :])
+        nc.sync.dma_start(out=b_bc[:], in_=wo_b.partition_broadcast(P))
+
+        e_sb = keep.tile([P, 2 * GROUP, S], BF16)
+        nc.vector.memset(e_sb[:], 0.0)
+        ident_bf = const.tile([P, P], BF16)
+        make_identity(nc, ident_bf[:])
+        ident_f32 = const.tile([P, P], F32)
+        make_identity(nc, ident_f32[:])
+        mask_f32 = const.tile([P, P], F32)
+        nc.gpsimd.memset(mask_f32[:], 0.0)
+        nc.gpsimd.affine_select(
+            out=mask_f32[:],
+            in_=mask_f32[:],
+            compare_op=ALU.is_ge,
+            fill=MASK_RAW,
+            base=0,
+            pattern=[[-1, P]],
+            channel_multiplier=1,
+        )
+        mask_bf = const.tile([P, P], BF16)
+        nc.vector.tensor_copy(out=mask_bf[:], in_=mask_f32[:])
+
+        q_t = keep.tile([P, H, S], BF16)
+        k_t = keep.tile([P, H, S], BF16)
+        v_codes = keep.tile([P, E], U32, align_bytes=64)
+        v_scales = keep.tile([P, E], U8, align_bytes=64)
+        w_codes = keep.tile([P, GROUPS, E], U32, align_bytes=64)
+        w_scales = keep.tile([P, GROUPS, E], U8, align_bytes=64)
+        ctx_codes = keep.tile([P, GROUPS, S], U32, align_bytes=64)
+        ctx_scales = keep.tile([P, GROUPS, S], U8, align_bytes=64)
+        out_rows = out.rearrange("b (i p) o -> (b i) p o", p=P)
+
+        s_banks = {}
+        shifts = {}
+        rowsums = {}
+        e_banks = {}
+        e_grouped = {}
+        e_quantised = {}
+        c_banks = {}
+        inverses = {}
+        contexts = {}
+        w_grouped = {}
+
+        def e_row(n, j):
+            return (n % 2) * GROUP + j
+
+        def turn_q_and_k(n):
+            i, g = steps[n]
+            bank = ps_turn.tile([P, 2, GROUP, P], BF16, tag="turn")
+            for side, rows in enumerate((q_sb, k_sb)):
+                for j in range(GROUP):
+                    h = g * GROUP + j
+                    nc.tensor.transpose(bank[:, side, j, :], rows[:, i, h * DH : (h + 1) * DH], ident_bf[:])
+            for side, turned in enumerate((q_t, k_t)):
+                nc.scalar.copy(out=turned[:, g * GROUP : (g + 1) * GROUP, i * P : (i + 1) * P], in_=bank[:, side])
+
+        def quantise_v(g):
+            cols = slice(g * CHUNK, (g + 1) * CHUNK)
+            v_grouped = work.tile([P, CHUNK, PACK], BF16, align_bytes=64)
+            nc.vector.tensor_copy(out=v_grouped[:], in_=v_sb[:, :, cols].rearrange("p a f -> p f a"))
+            nc.vector.quantize_mx(
+                out=v_codes[:, cols].bitcast(FP8X4),
+                scales=v_scales[:, cols],
+                in_=v_grouped[:].rearrange("p f a -> p (f a)"),
+            )
+
+        def turn_w(piece):
+            c, g = piece // GROUPS, piece % GROUPS
+            grouped = work.tile([P, CHUNK, PACK], BF16, tag="w_grouped", align_bytes=64)
+            words = grouped[:].rearrange("p o j -> p (o j)").bitcast(F32).rearrange("p (o u) -> p o u", u=2)
+            for half in range(2):
+                bank = ps_turn.tile([P, 2, 2, P], F32, tag="turn")
+                for u in range(2):
+                    for b in range(2):
+                        w_words = w_sb[:, 4 * c + 2 * half + b, :].bitcast(F32)
+                        first = 256 * g + 128 * u
+                        nc.tensor.transpose(bank[:, u, b, :], w_words[:, first : first + P], ident_f32[:])
+                dst = words[:, half * 2 * P : (half + 1) * 2 * P, :]
+                src = bank[:].rearrange("p u b o -> p (b o) u")
+                nc.scalar.copy(out=dst, in_=src)
+            w_grouped[piece] = grouped
+
+        def quantise_w(piece):
+            c, g = piece // GROUPS, piece % GROUPS
+            cols = slice(c * CHUNK, (c + 1) * CHUNK)
+            nc.vector.quantize_mx(
+                out=w_codes[:, g, cols].bitcast(FP8X4),
+                scales=w_scales[:, g, cols],
+                in_=w_grouped[piece][:].rearrange("p o j -> p (o j)"),
+            )
+
+        def raw_scores(n, j):
+            i, g = steps[n]
+            h = g * GROUP + j
+            keys = (i + 1) * P
+            s_ps = ps_scores.tile([P, S], F32, tag="bank")
+            nc.tensor.matmul(
+                out=s_ps[:, :keys], lhsT=q_t[:, h, i * P : (i + 1) * P], rhs=k_t[:, h, :keys], start=True, stop=False
+            )
+            nc.tensor.matmul(out=s_ps[:, i * P : keys], lhsT=ident_bf[:], rhs=mask_bf[:], start=False, stop=True)
+            top = small.tile([P, 1], F32)
+            nc.vector.reduce_max(out=top[:], in_=s_ps[:, :keys], axis=AXIS.X)
+            shift = small.tile([P, 1], F32)
+            nc.vector.tensor_scalar_mul(out=shift[:], in0=top[:], scalar1=-SCALE)
+            s_banks[n, j] = s_ps
+            shifts[n, j] = shift
+
+        def exponentials(n, j):
+            keys = (steps[n][0] + 1) * P
+            if j == 0:
+                rowsums[n] = small.tile([P, GROUP], F32, name="rowsum")
+            nc.scalar.activation(
+                out=e_sb[:, e_row(n, j), :keys],
+                in_=s_banks[n, j][:, :keys],
+                func=ACT.Exp,
+                bias=shifts[n, j][:],
+                scale=SCALE,
+                accum_out=rowsums[n][:, j : j + 1],
+            )
+
+        def turn_e(n, pair):
+            bank = ps_turn.tile([P, 2, 2, P], F32, tag="turn")
+            for c in range(2):
+                for j in range(2):
+                    words = e_sb[:, e_row(n, 2 * pair + j), :].bitcast(F32)
+                    nc.tensor.transpose(bank[:, c, j, :], words[:, c * P : (c + 1) * P], ident_f32[:])
+            e_banks[n, pair] = bank
+
+        def group_e(n, pair):
+            if pair == 0:
+                e_grouped[n] = work.tile([P, GROUP, P, PACK], BF16, name="e_grouped", bufs=2, align_bytes=64)
+            nc.scalar.copy(
+                out=e_grouped[n][:, 2 * pair : 2 * pair + 2].rearrange("p j t (c e) -> p (j t) c e", c=2),
+                in_=e_banks[n, pair][:]
+                .rearrange("p c j t -> p (c j t)")
+                .bitcast(BF16)
+                .rearrange("p (c r e) -> p r c e", c=2, e=2),
+            )
+
+        def quantise_e(n):
+            e_codes = work.tile([P, GROUP * P], U32, align_bytes=64)
+            e_scales = work.tile([P, GROUP * P], U8, align_bytes=64)
+            nc.vector.quantize_mx(
+                out=e_codes[:].bitcast(FP8X4),
+                scales=e_scales[:],
+                in_=e_grouped[n][:].rearrange("p j t a -> p (j t a)"),
+            )
+            e_quantised[n] = (e_codes, e_scales)
+
+        def invert_rowsums(n):
+            inverses[n] = small.tile([P, GROUP], F32, name="inverse")
+            nc.vector.reciprocal(out=inverses[n][:], in_=rowsums[n][:])
+            c_banks[n] = ps_ctx.tile([P, GROUP, P], F32, name="c_ps")
+            contexts[n] = work.tile([P, GROUP * DH], BF16, name="ctx_sb")
+
+        def first_product(n, j):
+            h = steps[n][1] * GROUP + j
+            e_codes, e_scales = e_quantised[n]
+            nc.tensor.matmul_mx(
+                out=c_banks[n][:, j, :],
+                lhsT=e_codes[:, j * P : (j + 1) * P].bitcast(FP8X4),
+                lhsT_scale=e_scales[:, j * P : (j + 1) * P],
+                rhs=v_codes[:, h * DH : (h + 1) * DH].bitcast(FP8X4),
+                rhs_scale=v_scales[:, h * DH : (h + 1) * DH],
+                start=True,
+                stop=True,
+            )
+
+        def normalise(n, j):
+            h = steps[n][1] * GROUP + j
+            nc.vector.scalar_tensor_tensor(
+                out=contexts[n][:, j * DH : (j + 1) * DH],
+                in0=c_banks[n][:, j, :],
+                scalar=inverses[n][:, j : j + 1],
+                in1=fm_bc[:, h * DH : (h + 1) * DH],
+                op0=ALU.mult,
+                op1=ALU.mult,
+            )
+
+        def turn_ctx(n):
+            bank = ps_turn.tile([P, 2, P], F32, tag="turn")
+            for c in range(2):
+                nc.tensor.transpose(bank[:, c, :], contexts[n][:].bitcast(F32)[:, c * P : (c + 1) * P], ident_f32[:])
+            return bank
+
+        def quantise_ctx(n, bank):
+            i, g = steps[n]
+            ctx_grouped = work.tile([P, P, PACK], BF16, align_bytes=64)
+            nc.vector.tensor_copy(
+                out=ctx_grouped[:].rearrange("p t (c e) -> p t c e", c=2),
+                in_=bank[:].rearrange("p c t -> p (c t)").bitcast(BF16).rearrange("p (c t e) -> p t c e", c=2, e=2),
+            )
+            nc.vector.quantize_mx(
+                out=ctx_codes[:, g, i * P : (i + 1) * P].bitcast(FP8X4),
+                scales=ctx_scales[:, g, i * P : (i + 1) * P],
+                in_=ctx_grouped[:].rearrange("p t a -> p (t a)"),
+            )
+
+        def project(i):
+            for c in range(CHUNKS):
+                cols = slice(c * CHUNK, (c + 1) * CHUNK)
+                acc = ps_scores.tile([P, CHUNK], F32, tag="bank")
+                for g in range(GROUPS):
+                    nc.tensor.matmul_mx(
+                        out=acc[:],
+                        lhsT=ctx_codes[:, g, i * P : (i + 1) * P].bitcast(FP8X4),
+                        lhsT_scale=ctx_scales[:, g, i * P : (i + 1) * P],
+                        rhs=w_codes[:, g, cols].bitcast(FP8X4),
+                        rhs_scale=w_scales[:, g, cols],
+                        start=(g == 0),
+                        stop=(g == GROUPS - 1),
+                    )
+                biased = work.tile([P, CHUNK], F32)
+                nc.vector.tensor_tensor(out=biased[:], in0=acc[:], in1=b_bc[:, cols], op=ALU.add)
+                result = work.tile([P, CHUNK], F32)
+                nc.gpsimd.tensor_tensor(out=result[:], in0=biased[:], in1=fm_bc[:, cols], op=ALU.mult)
+                nc.sync.dma_start(out=out_rows[i][:, cols], in_=result[:])
+
+        def valid(n):
+            return 0 <= n < len(steps)
+
+        w_done_round = W_FIRST_ROUND + (W_PIECES + W_PER_ROUND - 1) // W_PER_ROUND
+        project_in_round = {max(GROUPS * i + GROUPS + 2, w_done_round + i): i for i in range(BLOCKS)}
+
+        turn_q_and_k(0)
+        turn_q_and_k(1)
+        for n in range(len(steps) + 3):
+            if valid(n):
+                for j in range(GROUP):
+                    raw_scores(n, j)
+                    exponentials(n, j)
+            if valid(n - 3):
+                ctx_bank = turn_ctx(n - 3)
+            if valid(n - 1):
+                turn_e(n - 1, 0)
+                turn_e(n - 1, 1)
+                group_e(n - 1, 0)
+                group_e(n - 1, 1)
+            if valid(n - 2):
+                quantise_e(n - 2)
+            if valid(n - 3):
+                quantise_ctx(n - 3, ctx_bank)
+            for piece in range((n - 1 - W_FIRST_ROUND) * W_PER_ROUND, (n - W_FIRST_ROUND) * W_PER_ROUND):
+                if 0 <= piece < W_PIECES:
+                    quantise_w(piece)
+            if n < GROUPS:
+                quantise_v(n)
+            if valid(n - 2):
+                invert_rowsums(n - 2)
+                for j in range(GROUP):
+                    first_product(n - 2, j)
+                for j in range(GROUP):
+                    normalise(n - 2, j)
+            if valid(n + 2):
+                turn_q_and_k(n + 2)
+            for piece in range((n - W_FIRST_ROUND) * W_PER_ROUND, (n + 1 - W_FIRST_ROUND) * W_PER_ROUND):
+                if 0 <= piece < W_PIECES:
+                    turn_w(piece)
+            if n in project_in_round:
+                project(project_in_round[n])

@@ -33,19 +33,23 @@ FLOPS = 2 * H * S * S * DH * 2 + 2 * S * E * E
 W_PIECES = GROUPS * CHUNKS
 W_PER_ROUND = 2
 W_FIRST_ROUND = 3
+QK_LEAD = 3
 
 
 def tile_onedscaleparallelmha_pb_kernel(tc, q_rot, k_rot, v, feat_mask, wo_w, wo_b, out):
     nc = tc.nc
     steps = [(i, g) for i in range(BLOCKS) for g in range(GROUPS)]
 
+    def valid(n):
+        return 0 <= n < len(steps)
+
     with ExitStack() as stack:
         const = stack.enter_context(tc.tile_pool(name="const", bufs=1))
         keep = stack.enter_context(tc.tile_pool(name="keep", bufs=1))
         work = stack.enter_context(tc.tile_pool(name="work", bufs=3))
-        small = stack.enter_context(tc.tile_pool(name="small", bufs=8))
-        ps_scores = stack.enter_context(tc.psum_pool(name="ps_scores", bufs=4))
-        ps_turn = stack.enter_context(tc.psum_pool(name="ps_turn", bufs=3))
+        small = stack.enter_context(tc.tile_pool(name="small", bufs=12))
+        ps_scores = stack.enter_context(tc.psum_pool(name="ps_scores", bufs=3))
+        ps_turn = stack.enter_context(tc.psum_pool(name="ps_turn", bufs=4))
         ps_ctx = stack.enter_context(tc.psum_pool(name="ps_ctx", bufs=1))
         stack.enter_context(tc.manual_schedule())
 
@@ -102,7 +106,8 @@ def tile_onedscaleparallelmha_pb_kernel(tc, q_rot, k_rot, v, feat_mask, wo_w, wo
         ctx_scales = keep.tile([P, GROUPS, S], U8, align_bytes=64)
         out_rows = out.rearrange("b (i p) o -> (b i) p o", p=P)
 
-        s_banks = {}
+        qk_banks = {}
+        scaled_scores = {}
         shifts = {}
         rowsums = {}
         e_banks = {}
@@ -111,48 +116,77 @@ def tile_onedscaleparallelmha_pb_kernel(tc, q_rot, k_rot, v, feat_mask, wo_w, wo
         c_banks = {}
         inverses = {}
         contexts = {}
+        ctx_banks = {}
+        ctx_grouped = {}
+        v_grouped = {}
+        w_banks = {}
         w_grouped = {}
 
         def e_row(n, j):
             return (n % 2) * GROUP + j
 
+
         def turn_q_and_k(n):
+            if not valid(n):
+                return
             i, g = steps[n]
-            bank = ps_turn.tile([P, 2, GROUP, P], BF16, tag="turn")
+            qk_banks[n] = ps_turn.tile([P, 2, GROUP, P], BF16, name="qk_bank", tag="turn")
             for side, rows in enumerate((q_sb, k_sb)):
                 for j in range(GROUP):
                     h = g * GROUP + j
-                    nc.tensor.transpose(bank[:, side, j, :], rows[:, i, h * DH : (h + 1) * DH], ident_bf[:])
+                    nc.tensor.transpose(qk_banks[n][:, side, j, :], rows[:, i, h * DH : (h + 1) * DH], ident_bf[:])
+
+        def keep_q_and_k(n):
+            if not valid(n):
+                return
+            i, g = steps[n]
             for side, turned in enumerate((q_t, k_t)):
-                nc.scalar.copy(out=turned[:, g * GROUP : (g + 1) * GROUP, i * P : (i + 1) * P], in_=bank[:, side])
+                nc.scalar.copy(
+                    out=turned[:, g * GROUP : (g + 1) * GROUP, i * P : (i + 1) * P], in_=qk_banks[n][:, side]
+                )
+
+        def group_v(g):
+            if not 0 <= g < GROUPS:
+                return
+            cols = slice(g * CHUNK, (g + 1) * CHUNK)
+            v_grouped[g] = work.tile([P, CHUNK, PACK], BF16, name="v_grouped", tag="grouped", align_bytes=64)
+            nc.vector.tensor_copy(out=v_grouped[g][:], in_=v_sb[:, :, cols].rearrange("p a f -> p f a"))
 
         def quantise_v(g):
+            if not 0 <= g < GROUPS:
+                return
             cols = slice(g * CHUNK, (g + 1) * CHUNK)
-            v_grouped = work.tile([P, CHUNK, PACK], BF16, align_bytes=64)
-            nc.vector.tensor_copy(out=v_grouped[:], in_=v_sb[:, :, cols].rearrange("p a f -> p f a"))
             nc.vector.quantize_mx(
                 out=v_codes[:, cols].bitcast(FP8X4),
                 scales=v_scales[:, cols],
-                in_=v_grouped[:].rearrange("p f a -> p (f a)"),
+                in_=v_grouped[g][:].rearrange("p f a -> p (f a)"),
             )
 
-        def turn_w(piece):
+        def turn_w(piece, half):
+            if not 0 <= piece < W_PIECES:
+                return
             c, g = piece // GROUPS, piece % GROUPS
-            grouped = work.tile([P, CHUNK, PACK], BF16, tag="w_grouped", align_bytes=64)
-            words = grouped[:].rearrange("p o j -> p (o j)").bitcast(F32).rearrange("p (o u) -> p o u", u=2)
-            for half in range(2):
-                bank = ps_turn.tile([P, 2, 2, P], F32, tag="turn")
-                for u in range(2):
-                    for b in range(2):
-                        w_words = w_sb[:, 4 * c + 2 * half + b, :].bitcast(F32)
-                        first = 256 * g + 128 * u
-                        nc.tensor.transpose(bank[:, u, b, :], w_words[:, first : first + P], ident_f32[:])
-                dst = words[:, half * 2 * P : (half + 1) * 2 * P, :]
-                src = bank[:].rearrange("p u b o -> p (b o) u")
-                nc.scalar.copy(out=dst, in_=src)
-            w_grouped[piece] = grouped
+            w_banks[piece, half] = ps_turn.tile([P, 2, 2, P], F32, name="w_bank", tag="turn")
+            for u in range(2):
+                for b in range(2):
+                    w_words = w_sb[:, 4 * c + 2 * half + b, :].bitcast(F32)
+                    first = 256 * g + 128 * u
+                    nc.tensor.transpose(w_banks[piece, half][:, u, b, :], w_words[:, first : first + P], ident_f32[:])
+
+        def group_w(piece, half):
+            if not 0 <= piece < W_PIECES:
+                return
+            if half == 0:
+                w_grouped[piece] = work.tile([P, CHUNK, PACK], BF16, name="w_grouped", tag="grouped", align_bytes=64)
+            words = w_grouped[piece][:].rearrange("p o j -> p (o j)").bitcast(F32).rearrange("p (o u) -> p o u", u=2)
+            nc.scalar.copy(
+                out=words[:, half * 2 * P : (half + 1) * 2 * P, :],
+                in_=w_banks[piece, half][:].rearrange("p u b o -> p (b o) u"),
+            )
 
         def quantise_w(piece):
+            if not 0 <= piece < W_PIECES:
+                return
             c, g = piece // GROUPS, piece % GROUPS
             cols = slice(c * CHUNK, (c + 1) * CHUNK)
             nc.vector.quantize_mx(
@@ -161,7 +195,9 @@ def tile_onedscaleparallelmha_pb_kernel(tc, q_rot, k_rot, v, feat_mask, wo_w, wo
                 in_=w_grouped[piece][:].rearrange("p o j -> p (o j)"),
             )
 
-        def raw_scores(n, j):
+        def scores(n, j):
+            if not valid(n):
+                return
             i, g = steps[n]
             h = g * GROUP + j
             keys = (i + 1) * P
@@ -170,46 +206,62 @@ def tile_onedscaleparallelmha_pb_kernel(tc, q_rot, k_rot, v, feat_mask, wo_w, wo
                 out=s_ps[:, :keys], lhsT=q_t[:, h, i * P : (i + 1) * P], rhs=k_t[:, h, :keys], start=True, stop=False
             )
             nc.tensor.matmul(out=s_ps[:, i * P : keys], lhsT=ident_bf[:], rhs=mask_bf[:], start=False, stop=True)
-            top = small.tile([P, 1], F32)
-            nc.vector.reduce_max(out=top[:], in_=s_ps[:, :keys], axis=AXIS.X)
-            shift = small.tile([P, 1], F32)
-            nc.vector.tensor_scalar_mul(out=shift[:], in0=top[:], scalar1=-SCALE)
-            s_banks[n, j] = s_ps
-            shifts[n, j] = shift
+            scaled_scores[n, j] = work.tile([P, S], F32, name="scaled", bufs=2 * GROUP)
+            shifts[n, j] = small.tile([P, 1], F32, name="shift")
+            nc.vector.tensor_scalar(
+                out=scaled_scores[n, j][:, :keys],
+                in0=s_ps[:, :keys],
+                scalar1=-SCALE,
+                scalar2=None,
+                op0=ALU.mult,
+                op1=ALU.min,
+                accum_out=shifts[n, j][:],
+            )
 
         def exponentials(n, j):
+            if not valid(n):
+                return
             keys = (steps[n][0] + 1) * P
             if j == 0:
                 rowsums[n] = small.tile([P, GROUP], F32, name="rowsum")
             nc.scalar.activation(
                 out=e_sb[:, e_row(n, j), :keys],
-                in_=s_banks[n, j][:, :keys],
+                in_=scaled_scores[n, j][:, :keys],
                 func=ACT.Exp,
                 bias=shifts[n, j][:],
-                scale=SCALE,
+                scale=-1.0,
                 accum_out=rowsums[n][:, j : j + 1],
             )
 
         def turn_e(n, pair):
-            bank = ps_turn.tile([P, 2, 2, P], F32, tag="turn")
+            if not valid(n):
+                return
+            e_banks[n, pair] = ps_turn.tile([P, 2, 2, P], F32, name="e_bank", tag="turn")
             for c in range(2):
                 for j in range(2):
                     words = e_sb[:, e_row(n, 2 * pair + j), :].bitcast(F32)
-                    nc.tensor.transpose(bank[:, c, j, :], words[:, c * P : (c + 1) * P], ident_f32[:])
-            e_banks[n, pair] = bank
+                    nc.tensor.transpose(e_banks[n, pair][:, c, j, :], words[:, c * P : (c + 1) * P], ident_f32[:])
 
         def group_e(n, pair):
+            if not valid(n):
+                return
             if pair == 0:
                 e_grouped[n] = work.tile([P, GROUP, P, PACK], BF16, name="e_grouped", bufs=2, align_bytes=64)
-            nc.scalar.copy(
-                out=e_grouped[n][:, 2 * pair : 2 * pair + 2].rearrange("p j t (c e) -> p (j t) c e", c=2),
-                in_=e_banks[n, pair][:]
+            dst = e_grouped[n][:, 2 * pair : 2 * pair + 2].rearrange("p j t (c e) -> p (j t) c e", c=2)
+            src = (
+                e_banks[n, pair][:]
                 .rearrange("p c j t -> p (c j t)")
                 .bitcast(BF16)
-                .rearrange("p (c r e) -> p r c e", c=2, e=2),
+                .rearrange("p (c r e) -> p r c e", c=2, e=2)
             )
+            if pair == 0:
+                nc.scalar.copy(out=dst, in_=src)
+            else:
+                nc.vector.tensor_copy(out=dst, in_=src)
 
         def quantise_e(n):
+            if not valid(n):
+                return
             e_codes = work.tile([P, GROUP * P], U32, align_bytes=64)
             e_scales = work.tile([P, GROUP * P], U8, align_bytes=64)
             nc.vector.quantize_mx(
@@ -220,55 +272,76 @@ def tile_onedscaleparallelmha_pb_kernel(tc, q_rot, k_rot, v, feat_mask, wo_w, wo
             e_quantised[n] = (e_codes, e_scales)
 
         def invert_rowsums(n):
+            if not valid(n):
+                return
             inverses[n] = small.tile([P, GROUP], F32, name="inverse")
             nc.vector.reciprocal(out=inverses[n][:], in_=rowsums[n][:])
+
+        def first_product(n):
+            if not valid(n):
+                return
             c_banks[n] = ps_ctx.tile([P, GROUP, P], F32, name="c_ps")
-            contexts[n] = work.tile([P, GROUP * DH], BF16, name="ctx_sb")
-
-        def first_product(n, j):
-            h = steps[n][1] * GROUP + j
             e_codes, e_scales = e_quantised[n]
-            nc.tensor.matmul_mx(
-                out=c_banks[n][:, j, :],
-                lhsT=e_codes[:, j * P : (j + 1) * P].bitcast(FP8X4),
-                lhsT_scale=e_scales[:, j * P : (j + 1) * P],
-                rhs=v_codes[:, h * DH : (h + 1) * DH].bitcast(FP8X4),
-                rhs_scale=v_scales[:, h * DH : (h + 1) * DH],
-                start=True,
-                stop=True,
-            )
+            for j in range(GROUP):
+                h = steps[n][1] * GROUP + j
+                nc.tensor.matmul_mx(
+                    out=c_banks[n][:, j, :],
+                    lhsT=e_codes[:, j * P : (j + 1) * P].bitcast(FP8X4),
+                    lhsT_scale=e_scales[:, j * P : (j + 1) * P],
+                    rhs=v_codes[:, h * DH : (h + 1) * DH].bitcast(FP8X4),
+                    rhs_scale=v_scales[:, h * DH : (h + 1) * DH],
+                    start=True,
+                    stop=True,
+                )
 
-        def normalise(n, j):
-            h = steps[n][1] * GROUP + j
-            nc.vector.scalar_tensor_tensor(
-                out=contexts[n][:, j * DH : (j + 1) * DH],
-                in0=c_banks[n][:, j, :],
-                scalar=inverses[n][:, j : j + 1],
-                in1=fm_bc[:, h * DH : (h + 1) * DH],
-                op0=ALU.mult,
-                op1=ALU.mult,
-            )
+        def normalise(n):
+            if not valid(n):
+                return
+            contexts[n] = work.tile([P, GROUP * DH], BF16, name="ctx_sb")
+            for j in range(GROUP):
+                h = steps[n][1] * GROUP + j
+                nc.vector.scalar_tensor_tensor(
+                    out=contexts[n][:, j * DH : (j + 1) * DH],
+                    in0=c_banks[n][:, j, :],
+                    scalar=inverses[n][:, j : j + 1],
+                    in1=fm_bc[:, h * DH : (h + 1) * DH],
+                    op0=ALU.mult,
+                    op1=ALU.mult,
+                )
 
         def turn_ctx(n):
-            bank = ps_turn.tile([P, 2, P], F32, tag="turn")
+            if not valid(n):
+                return
+            ctx_banks[n] = ps_turn.tile([P, 2, P], F32, name="ctx_bank", tag="turn")
             for c in range(2):
-                nc.tensor.transpose(bank[:, c, :], contexts[n][:].bitcast(F32)[:, c * P : (c + 1) * P], ident_f32[:])
-            return bank
+                nc.tensor.transpose(
+                    ctx_banks[n][:, c, :], contexts[n][:].bitcast(F32)[:, c * P : (c + 1) * P], ident_f32[:]
+                )
 
-        def quantise_ctx(n, bank):
-            i, g = steps[n]
-            ctx_grouped = work.tile([P, P, PACK], BF16, align_bytes=64)
+        def group_ctx(n):
+            if not valid(n):
+                return
+            ctx_grouped[n] = work.tile([P, P, PACK], BF16, name="ctx_grouped", align_bytes=64)
             nc.vector.tensor_copy(
-                out=ctx_grouped[:].rearrange("p t (c e) -> p t c e", c=2),
-                in_=bank[:].rearrange("p c t -> p (c t)").bitcast(BF16).rearrange("p (c t e) -> p t c e", c=2, e=2),
+                out=ctx_grouped[n][:].rearrange("p t (c e) -> p t c e", c=2),
+                in_=ctx_banks[n][:]
+                .rearrange("p c t -> p (c t)")
+                .bitcast(BF16)
+                .rearrange("p (c t e) -> p t c e", c=2, e=2),
             )
+
+        def quantise_ctx(n):
+            if not valid(n):
+                return
+            i, g = steps[n]
             nc.vector.quantize_mx(
                 out=ctx_codes[:, g, i * P : (i + 1) * P].bitcast(FP8X4),
                 scales=ctx_scales[:, g, i * P : (i + 1) * P],
-                in_=ctx_grouped[:].rearrange("p t a -> p (t a)"),
+                in_=ctx_grouped[n][:].rearrange("p t a -> p (t a)"),
             )
 
         def project(i):
+            multiplier = nc.vector if i == BLOCKS - 1 else nc.gpsimd
             for c in range(CHUNKS):
                 cols = slice(c * CHUNK, (c + 1) * CHUNK)
                 acc = ps_scores.tile([P, CHUNK], F32, tag="bank")
@@ -285,48 +358,47 @@ def tile_onedscaleparallelmha_pb_kernel(tc, q_rot, k_rot, v, feat_mask, wo_w, wo
                 biased = work.tile([P, CHUNK], F32)
                 nc.vector.tensor_tensor(out=biased[:], in0=acc[:], in1=b_bc[:, cols], op=ALU.add)
                 result = work.tile([P, CHUNK], F32)
-                nc.gpsimd.tensor_tensor(out=result[:], in0=biased[:], in1=fm_bc[:, cols], op=ALU.mult)
+                multiplier.tensor_tensor(out=result[:], in0=biased[:], in1=fm_bc[:, cols], op=ALU.mult)
                 nc.sync.dma_start(out=out_rows[i][:, cols], in_=result[:])
-
-        def valid(n):
-            return 0 <= n < len(steps)
 
         w_done_round = W_FIRST_ROUND + (W_PIECES + W_PER_ROUND - 1) // W_PER_ROUND
         project_in_round = {max(GROUPS * i + GROUPS + 2, w_done_round + i): i for i in range(BLOCKS)}
 
-        turn_q_and_k(0)
-        turn_q_and_k(1)
-        for n in range(len(steps) + 3):
-            if valid(n):
-                for j in range(GROUP):
-                    raw_scores(n, j)
-                    exponentials(n, j)
-            if valid(n - 3):
-                ctx_bank = turn_ctx(n - 3)
-            if valid(n - 1):
-                turn_e(n - 1, 0)
-                turn_e(n - 1, 1)
-                group_e(n - 1, 0)
-                group_e(n - 1, 1)
-            if valid(n - 2):
-                quantise_e(n - 2)
-            if valid(n - 3):
-                quantise_ctx(n - 3, ctx_bank)
-            for piece in range((n - 1 - W_FIRST_ROUND) * W_PER_ROUND, (n - W_FIRST_ROUND) * W_PER_ROUND):
-                if 0 <= piece < W_PIECES:
-                    quantise_w(piece)
-            if n < GROUPS:
-                quantise_v(n)
-            if valid(n - 2):
-                invert_rowsums(n - 2)
-                for j in range(GROUP):
-                    first_product(n - 2, j)
-                for j in range(GROUP):
-                    normalise(n - 2, j)
-            if valid(n + 2):
-                turn_q_and_k(n + 2)
-            for piece in range((n - W_FIRST_ROUND) * W_PER_ROUND, (n + 1 - W_FIRST_ROUND) * W_PER_ROUND):
-                if 0 <= piece < W_PIECES:
-                    turn_w(piece)
+        for n in range(-QK_LEAD, len(steps) + 3):
+            first_piece = (n - W_FIRST_ROUND) * W_PER_ROUND
+            turn_e(n - 1, 0)
+            turn_e(n - 1, 1)
+            turn_ctx(n - 3)
+            turn_q_and_k(n + QK_LEAD)
+            quantise_e(n - 2)
+            group_ctx(n - 3)
+            invert_rowsums(n - 2)
+            quantise_v(n - 1)
+
+            exponentials(n, 0)
+            scores(n + 1, 0)
+            group_e(n - 1, 0)
+            quantise_ctx(n - 3)
+
+            exponentials(n, 1)
+            scores(n + 1, 1)
+            group_e(n - 1, 1)
+            first_product(n - 2)
+
+            exponentials(n, 2)
+            scores(n + 1, 2)
+            keep_q_and_k(n + QK_LEAD)
+
+            exponentials(n, 3)
+            scores(n + 1, 3)
+
+            normalise(n - 2)
+            for piece in range(first_piece - W_PER_ROUND, first_piece):
+                quantise_w(piece)
+            group_v(n)
+            for piece in range(first_piece, first_piece + W_PER_ROUND):
+                for half in range(2):
+                    turn_w(piece, half)
+                    group_w(piece, half)
             if n in project_in_round:
                 project(project_in_round[n])

@@ -60,21 +60,31 @@ def tile_onedscaleparallelmha_pb_kernel(tc, q_rot, k_rot, v, feat_mask, wo_w, wo
         k_sb = keep.tile([P, BLOCKS, E], BF16)
         v_sb = keep.tile([P, PACK, E], BF16)
         w_sb = keep.tile([P, H, E], BF16)
-        fm_bc = const.tile([P, E], BF16)
-        b_bc = const.tile([P, E], BF16)
-        for i, g in steps:
-            cols = slice(g * GROUP * DH, (g + 1) * GROUP * DH)
-            nc.sync.dma_start(out=q_sb[:, i, cols], in_=q_rows[i][:, cols])
-            nc.sync.dma_start(out=k_sb[:, i, cols], in_=k_rows[i][:, cols])
-            if (i, g) == (0, GROUPS - 1):
-                nc.sync.dma_start(
-                    out=v_sb[:].rearrange("p (c e) f -> p c (e f)", c=2),
-                    in_=v.rearrange("b (c p e) h d -> p (b c) (e h d)", c=2, e=2),
-                )
-                nc.sync.dma_start(out=fm_bc[:], in_=feat_mask.partition_broadcast(P))
-        for c in range(CHUNKS):
+        vector_rows = const.tile([P, 2, E], BF16)
+        nc.vector.memset(vector_rows[:], 0.0)
+
+        def load_q_and_k(i):
+            for g in range(GROUPS):
+                cols = slice(g * GROUP * DH, (g + 1) * GROUP * DH)
+                nc.sync.dma_start(out=q_sb[:, i, cols], in_=q_rows[i][:, cols])
+                nc.sync.dma_start(out=k_sb[:, i, cols], in_=k_rows[i][:, cols])
+
+        def load_w(c):
             nc.sync.dma_start(out=w_sb[:, 4 * c : 4 * c + 4, :], in_=w_rows[:, 4 * c : 4 * c + 4, :])
-        nc.sync.dma_start(out=b_bc[:], in_=wo_b.partition_broadcast(P))
+
+        load_q_and_k(0)
+        nc.sync.dma_start(out=vector_rows[0:1, 0, :], in_=feat_mask.unsqueeze(0))
+        nc.sync.dma_start(out=vector_rows[0:1, 1, :], in_=wo_b.unsqueeze(0))
+        nc.sync.dma_start(
+            out=v_sb[:].rearrange("p (c e) f -> p c (e f)", c=2),
+            in_=v.rearrange("b (c p e) h d -> p (b c) (e h d)", c=2, e=2),
+        )
+        load_q_and_k(1)
+        load_w(0)
+        load_q_and_k(2)
+        load_w(1)
+        load_w(2)
+        load_q_and_k(3)
 
         e_sb = keep.tile([P, 2 * GROUP, S], BF16)
         nc.vector.memset(e_sb[:], 0.0)
@@ -95,6 +105,10 @@ def tile_onedscaleparallelmha_pb_kernel(tc, q_rot, k_rot, v, feat_mask, wo_w, wo
         )
         mask_bf = const.tile([P, P], BF16)
         nc.vector.tensor_copy(out=mask_bf[:], in_=mask_f32[:])
+        ones_bf = const.tile([P, P], BF16)
+        nc.vector.memset(ones_bf[:], 1.0)
+        fm_bc = const.tile([P, E], BF16)
+        b_bc = const.tile([P, E], BF16)
 
         q_t = keep.tile([P, H, S], BF16)
         k_t = keep.tile([P, H, S], BF16)
@@ -125,6 +139,15 @@ def tile_onedscaleparallelmha_pb_kernel(tc, q_rot, k_rot, v, feat_mask, wo_w, wo
         def e_row(n, j):
             return (n % 2) * GROUP + j
 
+
+        def spread_over_partitions(k):
+            if not 0 <= k < 2:
+                return
+            for c in range(CHUNKS):
+                cols = slice(c * CHUNK, (c + 1) * CHUNK)
+                repeated = ps_scores.tile([P, CHUNK], F32, tag="bank")
+                nc.tensor.matmul(out=repeated[:], lhsT=ones_bf[:], rhs=vector_rows[:, k, cols], start=True, stop=True)
+                nc.scalar.copy(out=(fm_bc, b_bc)[k][:, cols], in_=repeated[:])
 
         def turn_q_and_k(n):
             if not valid(n):
@@ -391,6 +414,7 @@ def tile_onedscaleparallelmha_pb_kernel(tc, q_rot, k_rot, v, feat_mask, wo_w, wo
 
             exponentials(n, 3)
             scores(n + 1, 3)
+            spread_over_partitions(n + QK_LEAD - 1)
 
             normalise(n - 2)
             for piece in range(first_piece - W_PER_ROUND, first_piece):

@@ -7,6 +7,7 @@ from concourse.masks import make_identity
 BF16 = mybir.dt.bfloat16
 F32 = mybir.dt.float32
 U32 = mybir.dt.uint32
+I32 = mybir.dt.int32
 U8 = mybir.dt.uint8
 FP8X4 = mybir.dt.float8_e4m3fn_x4
 ALU = mybir.AluOpType
@@ -33,7 +34,7 @@ FLOPS = 2 * H * S * S * DH * 2 + 2 * S * E * E
 W_PIECES = GROUPS * CHUNKS
 W_PER_ROUND = 2
 W_FIRST_ROUND = 3
-QK_LEAD = 3
+QK_LEAD = 2
 
 
 def tile_onedscaleparallelmha_pb_kernel(tc, q_rot, k_rot, v, feat_mask, wo_w, wo_b, out):
@@ -61,7 +62,7 @@ def tile_onedscaleparallelmha_pb_kernel(tc, q_rot, k_rot, v, feat_mask, wo_w, wo
         v_sb = keep.tile([P, PACK, E], BF16)
         w_sb = keep.tile([P, H, E], BF16)
         vector_rows = const.tile([P, 2, E], BF16)
-        nc.vector.memset(vector_rows[:], 0.0)
+        nc.vector.memset(vector_rows[:].rearrange("p k f -> p (k f)").bitcast(I32), 0)
 
         def load_q_and_k(i):
             for g in range(GROUPS):
@@ -87,7 +88,7 @@ def tile_onedscaleparallelmha_pb_kernel(tc, q_rot, k_rot, v, feat_mask, wo_w, wo
         load_q_and_k(3)
 
         e_sb = keep.tile([P, 2 * GROUP, S], BF16)
-        nc.vector.memset(e_sb[:], 0.0)
+        nc.vector.memset(e_sb[:].rearrange("p r u -> p (r u)").bitcast(I32), 0)
         ident_bf = const.tile([P, P], BF16)
         make_identity(nc, ident_bf[:])
         ident_f32 = const.tile([P, P], F32)
@@ -107,11 +108,13 @@ def tile_onedscaleparallelmha_pb_kernel(tc, q_rot, k_rot, v, feat_mask, wo_w, wo
         nc.vector.tensor_copy(out=mask_bf[:], in_=mask_f32[:])
         ones_bf = const.tile([P, P], BF16)
         nc.vector.memset(ones_bf[:], 1.0)
-        fm_bc = const.tile([P, E], BF16)
-        b_bc = const.tile([P, E], BF16)
+        repeated_rows = const.tile([P, 2 * E], BF16)
+        fm_bc = repeated_rows[:, :E]
+        b_bc = repeated_rows[:, E:]
 
-        q_t = keep.tile([P, H, S], BF16)
-        k_t = keep.tile([P, H, S], BF16)
+        qk_t = keep.tile([P, 2, H, S], BF16)
+        q_t = qk_t[:, 0]
+        k_t = qk_t[:, 1]
         v_codes = keep.tile([P, E], U32, align_bytes=64)
         v_scales = keep.tile([P, E], U8, align_bytes=64)
         w_codes = keep.tile([P, GROUPS, E], U32, align_bytes=64)
@@ -135,19 +138,27 @@ def tile_onedscaleparallelmha_pb_kernel(tc, q_rot, k_rot, v, feat_mask, wo_w, wo
         v_grouped = {}
         w_banks = {}
         w_grouped = {}
+        out_banks = {}
 
         def e_row(n, j):
             return (n % 2) * GROUP + j
 
 
         def spread_over_partitions(k):
-            if not 0 <= k < 2:
+            if not 0 <= k < 2 * E // (2 * CHUNK):
                 return
-            for c in range(CHUNKS):
-                cols = slice(c * CHUNK, (c + 1) * CHUNK)
-                repeated = ps_scores.tile([P, CHUNK], F32, tag="bank")
-                nc.tensor.matmul(out=repeated[:], lhsT=ones_bf[:], rhs=vector_rows[:, k, cols], start=True, stop=True)
-                nc.scalar.copy(out=(fm_bc, b_bc)[k][:, cols], in_=repeated[:])
+            rows = vector_rows[:].rearrange("p k f -> p (k f)")
+            repeated = ps_scores.tile([P, 2 * CHUNK], BF16, tag="bank")
+            for half in range(2):
+                first = (2 * k + half) * CHUNK
+                nc.tensor.matmul(
+                    out=repeated[:, half * CHUNK : (half + 1) * CHUNK],
+                    lhsT=ones_bf[:],
+                    rhs=rows[:, first : first + CHUNK],
+                    start=True,
+                    stop=True,
+                )
+            nc.scalar.copy(out=repeated_rows[:, 2 * k * CHUNK : 2 * (k + 1) * CHUNK], in_=repeated[:])
 
         def turn_q_and_k(n):
             if not valid(n):
@@ -163,10 +174,7 @@ def tile_onedscaleparallelmha_pb_kernel(tc, q_rot, k_rot, v, feat_mask, wo_w, wo
             if not valid(n):
                 return
             i, g = steps[n]
-            for side, turned in enumerate((q_t, k_t)):
-                nc.scalar.copy(
-                    out=turned[:, g * GROUP : (g + 1) * GROUP, i * P : (i + 1) * P], in_=qk_banks[n][:, side]
-                )
+            nc.scalar.copy(out=qk_t[:, :, g * GROUP : (g + 1) * GROUP, i * P : (i + 1) * P], in_=qk_banks[n][:])
 
         def group_v(g):
             if not 0 <= g < GROUPS:
@@ -277,10 +285,7 @@ def tile_onedscaleparallelmha_pb_kernel(tc, q_rot, k_rot, v, feat_mask, wo_w, wo
                 .bitcast(BF16)
                 .rearrange("p (c r e) -> p r c e", c=2, e=2)
             )
-            if pair == 0:
-                nc.scalar.copy(out=dst, in_=src)
-            else:
-                nc.vector.tensor_copy(out=dst, in_=src)
+            nc.scalar.copy(out=dst, in_=src)
 
         def quantise_e(n):
             if not valid(n):
@@ -363,14 +368,16 @@ def tile_onedscaleparallelmha_pb_kernel(tc, q_rot, k_rot, v, feat_mask, wo_w, wo
                 in_=ctx_grouped[n][:].rearrange("p t a -> p (t a)"),
             )
 
-        def project(i):
-            multiplier = nc.vector if i == BLOCKS - 1 else nc.gpsimd
-            for c in range(CHUNKS):
-                cols = slice(c * CHUNK, (c + 1) * CHUNK)
-                acc = ps_scores.tile([P, CHUNK], F32, tag="bank")
-                for g in range(GROUPS):
+        def project(i, groups):
+            if not 0 <= i < BLOCKS:
+                return
+            for g in groups:
+                for c in range(CHUNKS):
+                    if g == 0:
+                        out_banks[i, c] = ps_scores.tile([P, CHUNK], F32, name="out_bank", tag="bank")
+                    cols = slice(c * CHUNK, (c + 1) * CHUNK)
                     nc.tensor.matmul_mx(
-                        out=acc[:],
+                        out=out_banks[i, c][:],
                         lhsT=ctx_codes[:, g, i * P : (i + 1) * P].bitcast(FP8X4),
                         lhsT_scale=ctx_scales[:, g, i * P : (i + 1) * P],
                         rhs=w_codes[:, g, cols].bitcast(FP8X4),
@@ -378,14 +385,21 @@ def tile_onedscaleparallelmha_pb_kernel(tc, q_rot, k_rot, v, feat_mask, wo_w, wo
                         start=(g == 0),
                         stop=(g == GROUPS - 1),
                     )
+
+        def finish(i):
+            if not 0 <= i < BLOCKS:
+                return
+            multiplier = nc.vector if i == BLOCKS - 1 else nc.gpsimd
+            for c in range(CHUNKS):
+                cols = slice(c * CHUNK, (c + 1) * CHUNK)
                 biased = work.tile([P, CHUNK], F32)
-                nc.vector.tensor_tensor(out=biased[:], in0=acc[:], in1=b_bc[:, cols], op=ALU.add)
+                nc.vector.tensor_tensor(out=biased[:], in0=out_banks[i, c][:], in1=b_bc[:, cols], op=ALU.add)
                 result = work.tile([P, CHUNK], F32)
                 multiplier.tensor_tensor(out=result[:], in0=biased[:], in1=fm_bc[:, cols], op=ALU.mult)
                 nc.sync.dma_start(out=out_rows[i][:, cols], in_=result[:])
 
         w_done_round = W_FIRST_ROUND + (W_PIECES + W_PER_ROUND - 1) // W_PER_ROUND
-        project_in_round = {max(GROUPS * i + GROUPS + 2, w_done_round + i): i for i in range(BLOCKS)}
+        project_in_round = {max(GROUPS * i + GROUPS + 2, w_done_round + i): i for i in range(BLOCKS - 1)}
 
         for n in range(-QK_LEAD, len(steps) + 3):
             first_piece = (n - W_FIRST_ROUND) * W_PER_ROUND
@@ -414,7 +428,7 @@ def tile_onedscaleparallelmha_pb_kernel(tc, q_rot, k_rot, v, feat_mask, wo_w, wo
 
             exponentials(n, 3)
             scores(n + 1, 3)
-            spread_over_partitions(n + QK_LEAD - 1)
+            spread_over_partitions(n)
 
             normalise(n - 2)
             for piece in range(first_piece - W_PER_ROUND, first_piece):
@@ -424,5 +438,11 @@ def tile_onedscaleparallelmha_pb_kernel(tc, q_rot, k_rot, v, feat_mask, wo_w, wo
                 for half in range(2):
                     turn_w(piece, half)
                     group_w(piece, half)
-            if n in project_in_round:
-                project(project_in_round[n])
+            if n + 1 == len(steps) + 2:
+                project(BLOCKS - 1, range(GROUPS - 1))
+            elif n == len(steps) + 2:
+                project(BLOCKS - 1, [GROUPS - 1])
+                finish(BLOCKS - 1)
+            elif n in project_in_round:
+                project(project_in_round[n], range(GROUPS))
+                finish(project_in_round[n])

@@ -278,14 +278,12 @@ def tile_onedscaleparallelmha_pb_kernel(tc, q_rot, k_rot, v, feat_mask, wo_w, wo
                 return
             if pair == 0:
                 e_grouped[n] = work.tile([P, GROUP, P, PACK], BF16, name="e_grouped", bufs=2, align_bytes=64)
-            dst = e_grouped[n][:, 2 * pair : 2 * pair + 2].rearrange("p j t (c e) -> p (j t) c e", c=2)
-            src = (
-                e_banks[n, pair][:]
-                .rearrange("p c j t -> p (c j t)")
-                .bitcast(BF16)
-                .rearrange("p (c r e) -> p r c e", c=2, e=2)
+            words = e_grouped[n][:].rearrange("p j t a -> p (j t a)").bitcast(F32)
+            words = words.rearrange("p (r c) -> p r c", c=2)
+            nc.scalar.copy(
+                out=words[:, pair * 2 * P : (pair + 1) * 2 * P, :],
+                in_=e_banks[n, pair][:].rearrange("p c j t -> p (j t) c"),
             )
-            nc.scalar.copy(out=dst, in_=src)
 
         def quantise_e(n):
             if not valid(n):
@@ -351,11 +349,8 @@ def tile_onedscaleparallelmha_pb_kernel(tc, q_rot, k_rot, v, feat_mask, wo_w, wo
                 return
             ctx_grouped[n] = work.tile([P, P, PACK], BF16, name="ctx_grouped", align_bytes=64)
             nc.vector.tensor_copy(
-                out=ctx_grouped[n][:].rearrange("p t (c e) -> p t c e", c=2),
-                in_=ctx_banks[n][:]
-                .rearrange("p c t -> p (c t)")
-                .bitcast(BF16)
-                .rearrange("p (c t e) -> p t c e", c=2, e=2),
+                out=ctx_grouped[n][:].rearrange("p t a -> p (t a)").bitcast(F32).rearrange("p (t c) -> p t c", c=2),
+                in_=ctx_banks[n][:].rearrange("p c t -> p t c"),
             )
 
         def quantise_ctx(n):

@@ -32,14 +32,17 @@ FLOPS = 2 * H * S * S * DH * 2 + 2 * S * E * E
 
 
 W_PIECES = GROUPS * CHUNKS
-W_PER_ROUND = 2
-W_FIRST_ROUND = 3
+W_HALVES_PER_ROUND = 3
+W_FIRST_ROUND = 2
+V_ON_SCALAR = ()
 QK_LEAD = 2
+BLOCK_ORDER = (0, 3, 2, 1)
+QK_UNITS = {0: (((0, 0), (1, 0)),), 3: (((1, 1), (1, 2)), ((0, 3), (1, 3))), 2: (((0, 1), (0, 2)),), 1: ()}
 
 
 def tile_onedscaleparallelmha_pb_kernel(tc, q_rot, k_rot, v, feat_mask, wo_w, wo_b, out):
     nc = tc.nc
-    steps = [(i, g) for i in range(BLOCKS) for g in range(GROUPS)]
+    steps = [(i, g) for i in BLOCK_ORDER for g in range(GROUPS)]
 
     def valid(n):
         return 0 <= n < len(steps)
@@ -49,8 +52,8 @@ def tile_onedscaleparallelmha_pb_kernel(tc, q_rot, k_rot, v, feat_mask, wo_w, wo
         keep = stack.enter_context(tc.tile_pool(name="keep", bufs=1))
         work = stack.enter_context(tc.tile_pool(name="work", bufs=3))
         small = stack.enter_context(tc.tile_pool(name="small", bufs=12))
-        ps_scores = stack.enter_context(tc.psum_pool(name="ps_scores", bufs=3))
-        ps_turn = stack.enter_context(tc.psum_pool(name="ps_turn", bufs=4))
+        ps_scores = stack.enter_context(tc.psum_pool(name="ps_scores", bufs=4))
+        ps_turn = stack.enter_context(tc.psum_pool(name="ps_turn", bufs=3))
         ps_ctx = stack.enter_context(tc.psum_pool(name="ps_ctx", bufs=1))
         stack.enter_context(tc.manual_schedule())
 
@@ -64,28 +67,31 @@ def tile_onedscaleparallelmha_pb_kernel(tc, q_rot, k_rot, v, feat_mask, wo_w, wo
         vector_rows = const.tile([P, 2, E], BF16)
         nc.vector.memset(vector_rows[:].rearrange("p k f -> p (k f)").bitcast(I32), 0)
 
-        def load_q_and_k(i):
-            for g in range(GROUPS):
-                cols = slice(g * GROUP * DH, (g + 1) * GROUP * DH)
-                nc.sync.dma_start(out=q_sb[:, i, cols], in_=q_rows[i][:, cols])
-                nc.sync.dma_start(out=k_sb[:, i, cols], in_=k_rows[i][:, cols])
+        def load(rows, sb, i, groups):
+            cols = slice(groups[0] * GROUP * DH, (groups[-1] + 1) * GROUP * DH)
+            nc.sync.dma_start(out=sb[:, i, cols], in_=rows[i][:, cols])
 
+        ALL = range(GROUPS)
         def load_w(c):
             nc.sync.dma_start(out=w_sb[:, 4 * c : 4 * c + 4, :], in_=w_rows[:, 4 * c : 4 * c + 4, :])
 
-        load_q_and_k(0)
+        for g in range(GROUPS):
+            load(q_rows, q_sb, 0, [g])
+            load(k_rows, k_sb, 0, [g])
         nc.sync.dma_start(out=vector_rows[0:1, 0, :], in_=feat_mask.unsqueeze(0))
         nc.sync.dma_start(out=vector_rows[0:1, 1, :], in_=wo_b.unsqueeze(0))
         nc.sync.dma_start(
             out=v_sb[:].rearrange("p (c e) f -> p c (e f)", c=2),
             in_=v.rearrange("b (c p e) h d -> p (b c) (e h d)", c=2, e=2),
         )
-        load_q_and_k(1)
+        for i in (1, 2, 3):
+            load(k_rows, k_sb, i, ALL)
+        load(q_rows, q_sb, 3, ALL)
         load_w(0)
-        load_q_and_k(2)
+        load(q_rows, q_sb, 2, ALL)
+        load(q_rows, q_sb, 1, ALL)
         load_w(1)
         load_w(2)
-        load_q_and_k(3)
 
         e_sb = keep.tile([P, 2 * GROUP, S], BF16)
         nc.vector.memset(e_sb[:].rearrange("p r u -> p (r u)").bitcast(I32), 0)
@@ -124,6 +130,7 @@ def tile_onedscaleparallelmha_pb_kernel(tc, q_rot, k_rot, v, feat_mask, wo_w, wo
         out_rows = out.rearrange("b (i p) o -> (b i) p o", p=P)
 
         qk_banks = {}
+        score_banks = {}
         scaled_scores = {}
         shifts = {}
         rowsums = {}
@@ -139,6 +146,7 @@ def tile_onedscaleparallelmha_pb_kernel(tc, q_rot, k_rot, v, feat_mask, wo_w, wo
         w_banks = {}
         w_grouped = {}
         out_banks = {}
+        biased = {}
 
         def e_row(n, j):
             return (n % 2) * GROUP + j
@@ -160,28 +168,39 @@ def tile_onedscaleparallelmha_pb_kernel(tc, q_rot, k_rot, v, feat_mask, wo_w, wo
                 )
             nc.scalar.copy(out=repeated_rows[:, 2 * k * CHUNK : 2 * (k + 1) * CHUNK], in_=repeated[:])
 
-        def turn_q_and_k(n):
-            if not valid(n):
+        def qk_units(n):
+            return QK_UNITS[steps[n][0]] if valid(n) else ()
+
+        def turn_q_and_k(n, u):
+            if u >= len(qk_units(n)):
                 return
-            i, g = steps[n]
-            qk_banks[n] = ps_turn.tile([P, 2, GROUP, P], BF16, name="qk_bank", tag="turn")
-            for side, rows in enumerate((q_sb, k_sb)):
+            g = steps[n][1]
+            qk_banks[n, u] = ps_turn.tile([P, 2, GROUP, P], BF16, name="qk_bank", tag="turn")
+            for slot, (side, i) in enumerate(qk_units(n)[u]):
+                rows = (q_sb, k_sb)[side]
                 for j in range(GROUP):
                     h = g * GROUP + j
-                    nc.tensor.transpose(qk_banks[n][:, side, j, :], rows[:, i, h * DH : (h + 1) * DH], ident_bf[:])
+                    nc.tensor.transpose(qk_banks[n, u][:, slot, j, :], rows[:, i, h * DH : (h + 1) * DH], ident_bf[:])
 
-        def keep_q_and_k(n):
-            if not valid(n):
+        def keep_q_and_k(n, u):
+            if u >= len(qk_units(n)):
                 return
-            i, g = steps[n]
-            nc.scalar.copy(out=qk_t[:, :, g * GROUP : (g + 1) * GROUP, i * P : (i + 1) * P], in_=qk_banks[n][:])
+            g = steps[n][1]
+            heads = slice(g * GROUP, (g + 1) * GROUP)
+            (side, i), (other, i2) = qk_units(n)[u]
+            if side == other:
+                dst = qk_t[:, side, heads, i * P : (i + 2) * P].rearrange("p h (b t) -> p b h t", b=2)
+            else:
+                dst = qk_t[:, :, heads, i * P : (i + 1) * P]
+            nc.scalar.copy(out=dst, in_=qk_banks[n, u][:])
 
         def group_v(g):
             if not 0 <= g < GROUPS:
                 return
+            move = nc.scalar.copy if g in V_ON_SCALAR else nc.vector.tensor_copy
             cols = slice(g * CHUNK, (g + 1) * CHUNK)
-            v_grouped[g] = work.tile([P, CHUNK, PACK], BF16, name="v_grouped", tag="grouped", align_bytes=64)
-            nc.vector.tensor_copy(out=v_grouped[g][:], in_=v_sb[:, :, cols].rearrange("p a f -> p f a"))
+            v_grouped[g] = work.tile([P, CHUNK, PACK], BF16, name="v_grouped", tag="v_grouped", bufs=2, align_bytes=64)
+            move(out=v_grouped[g][:], in_=v_sb[:, :, cols].rearrange("p a f -> p f a"))
 
         def quantise_v(g):
             if not 0 <= g < GROUPS:
@@ -232,11 +251,18 @@ def tile_onedscaleparallelmha_pb_kernel(tc, q_rot, k_rot, v, feat_mask, wo_w, wo
             i, g = steps[n]
             h = g * GROUP + j
             keys = (i + 1) * P
-            s_ps = ps_scores.tile([P, S], F32, tag="bank")
+            s_ps = ps_scores.tile([P, S], F32, name="score_bank", tag="bank")
+            score_banks[n, j] = s_ps
             nc.tensor.matmul(
                 out=s_ps[:, :keys], lhsT=q_t[:, h, i * P : (i + 1) * P], rhs=k_t[:, h, :keys], start=True, stop=False
             )
             nc.tensor.matmul(out=s_ps[:, i * P : keys], lhsT=ident_bf[:], rhs=mask_bf[:], start=False, stop=True)
+
+        def maxima(n, j):
+            if not valid(n):
+                return
+            keys = (steps[n][0] + 1) * P
+            s_ps = score_banks[n, j]
             scaled_scores[n, j] = work.tile([P, S], F32, name="scaled", bufs=2 * GROUP)
             shifts[n, j] = small.tile([P, 1], F32, name="shift")
             nc.vector.tensor_scalar(
@@ -263,6 +289,14 @@ def tile_onedscaleparallelmha_pb_kernel(tc, q_rot, k_rot, v, feat_mask, wo_w, wo
                 scale=-1.0,
                 accum_out=rowsums[n][:, j : j + 1],
             )
+
+        def clear_e(n):
+            if not valid(n) or not valid(n - 2):
+                return
+            i, before = steps[n][0], steps[n - 2][0]
+            if before > i:
+                rows = slice(e_row(n, 0), e_row(n, 0) + GROUP)
+                nc.gpsimd.memset(e_sb[:, rows, (i + 1) * P : (before + 1) * P].bitcast(I32), 0)
 
         def turn_e(n, pair):
             if not valid(n):
@@ -363,81 +397,147 @@ def tile_onedscaleparallelmha_pb_kernel(tc, q_rot, k_rot, v, feat_mask, wo_w, wo
                 in_=ctx_grouped[n][:].rearrange("p t a -> p (t a)"),
             )
 
-        def project(i, groups):
+        def project(i, c, groups):
             if not 0 <= i < BLOCKS:
                 return
+            if groups[0] == 0:
+                out_banks[i, c] = ps_scores.tile([P, CHUNK], F32, name="out_bank", tag="bank")
+            cols = slice(c * CHUNK, (c + 1) * CHUNK)
             for g in groups:
-                for c in range(CHUNKS):
-                    if g == 0:
-                        out_banks[i, c] = ps_scores.tile([P, CHUNK], F32, name="out_bank", tag="bank")
-                    cols = slice(c * CHUNK, (c + 1) * CHUNK)
-                    nc.tensor.matmul_mx(
-                        out=out_banks[i, c][:],
-                        lhsT=ctx_codes[:, g, i * P : (i + 1) * P].bitcast(FP8X4),
-                        lhsT_scale=ctx_scales[:, g, i * P : (i + 1) * P],
-                        rhs=w_codes[:, g, cols].bitcast(FP8X4),
-                        rhs_scale=w_scales[:, g, cols],
-                        start=(g == 0),
-                        stop=(g == GROUPS - 1),
-                    )
+                nc.tensor.matmul_mx(
+                    out=out_banks[i, c][:],
+                    lhsT=ctx_codes[:, g, i * P : (i + 1) * P].bitcast(FP8X4),
+                    lhsT_scale=ctx_scales[:, g, i * P : (i + 1) * P],
+                    rhs=w_codes[:, g, cols].bitcast(FP8X4),
+                    rhs_scale=w_scales[:, g, cols],
+                    start=(g == 0),
+                    stop=(g == GROUPS - 1),
+                )
 
-        def finish(i):
+        def add_bias(i, c):
             if not 0 <= i < BLOCKS:
                 return
-            multiplier = nc.vector if i == BLOCKS - 1 else nc.gpsimd
-            for c in range(CHUNKS):
-                cols = slice(c * CHUNK, (c + 1) * CHUNK)
-                biased = work.tile([P, CHUNK], F32)
-                nc.vector.tensor_tensor(out=biased[:], in0=out_banks[i, c][:], in1=b_bc[:, cols], op=ALU.add)
-                result = work.tile([P, CHUNK], F32)
-                multiplier.tensor_tensor(out=result[:], in0=biased[:], in1=fm_bc[:, cols], op=ALU.mult)
-                nc.sync.dma_start(out=out_rows[i][:, cols], in_=result[:])
+            biased[i, c] = work.tile([P, CHUNK], F32, name="biased")
+            nc.vector.tensor_tensor(
+                out=biased[i, c][:], in0=out_banks[i, c][:], in1=b_bc[:, c * CHUNK : (c + 1) * CHUNK], op=ALU.add
+            )
 
-        w_done_round = W_FIRST_ROUND + (W_PIECES + W_PER_ROUND - 1) // W_PER_ROUND
-        project_in_round = {max(GROUPS * i + GROUPS + 2, w_done_round + i): i for i in range(BLOCKS - 1)}
+        def scale_and_store(i, c, engine):
+            if not 0 <= i < BLOCKS:
+                return
+            cols = slice(c * CHUNK, (c + 1) * CHUNK)
+            result = work.tile([P, CHUNK], F32, name="result")
+            engine.tensor_tensor(out=result[:], in0=biased[i, c][:], in1=fm_bc[:, cols], op=ALU.mult)
+            nc.sync.dma_start(out=out_rows[i][:, cols], in_=result[:])
 
-        for n in range(-QK_LEAD, len(steps) + 3):
-            first_piece = (n - W_FIRST_ROUND) * W_PER_ROUND
+        finished = {6: [(0, 0)], 7: [(0, 1)], 9: [(1, 0), (0, 2)], 10: [(1, 1)], 11: [(1, 2)]}
+
+        def chunk_of(n, k):
+            found = finished.get(n, [])
+            return (BLOCK_ORDER[found[k][0]], found[k][1]) if k < len(found) else (-1, 0)
+
+        def halves_of(n):
+            return range((n - W_FIRST_ROUND) * W_HALVES_PER_ROUND, (n - W_FIRST_ROUND + 1) * W_HALVES_PER_ROUND)
+
+        def turn_half(half):
+            turn_w(half // 2, half % 2)
+
+        def group_half(half):
+            group_w(half // 2, half % 2)
+
+        def quantise_done(n, k):
+            done = [half // 2 for half in halves_of(n) if half % 2 == 1]
+            if k < len(done):
+                quantise_w(done[k])
+
+        for n in range(-QK_LEAD - 1, len(steps)):
+            halves = halves_of(n)
+            scores(n + 1, 1)
             turn_e(n - 1, 0)
             turn_e(n - 1, 1)
-            turn_ctx(n - 3)
-            turn_q_and_k(n + QK_LEAD)
+            clear_e(n)
             quantise_e(n - 2)
-            group_ctx(n - 3)
-            invert_rowsums(n - 2)
-            quantise_v(n - 1)
-
-            exponentials(n, 0)
-            scores(n + 1, 0)
-            group_e(n - 1, 0)
             quantise_ctx(n - 3)
+            quantise_done(n - 1, 0)
+            quantise_v(n - 1)
+            maxima(n + 1, 0)
+            invert_rowsums(n - 2)
+            add_bias(*chunk_of(n, 0))
+            exponentials(n, 0)
+            keep_q_and_k(n + QK_LEAD, 0)
+            scale_and_store(*chunk_of(n, 0), nc.gpsimd)
 
-            exponentials(n, 1)
-            scores(n + 1, 1)
-            group_e(n - 1, 1)
             first_product(n - 2)
-
-            exponentials(n, 2)
+            project(*chunk_of(n, 1), ALL)
             scores(n + 1, 2)
-            keep_q_and_k(n + QK_LEAD)
-
-            exponentials(n, 3)
-            scores(n + 1, 3)
-            spread_over_partitions(n)
-
+            turn_q_and_k(n + QK_LEAD, 1)
+            maxima(n + 1, 1)
             normalise(n - 2)
-            for piece in range(first_piece - W_PER_ROUND, first_piece):
-                quantise_w(piece)
+            exponentials(n, 1)
+            group_e(n - 1, 0)
+
+            turn_half(halves[0])
+            scores(n + 1, 3)
+            exponentials(n, 2)
+            group_e(n - 1, 1)
+            keep_q_and_k(n + QK_LEAD, 1)
+            turn_ctx(n - 2)
+            maxima(n + 1, 2)
+            add_bias(*chunk_of(n, 1))
+            scale_and_store(*chunk_of(n, 1), nc.gpsimd)
+            group_half(halves[0])
+
+            turn_half(halves[1])
+            spread_over_partitions(n)
+            scores(n + 2, 0)
+            turn_half(halves[2])
+            maxima(n + 1, 3)
+            group_ctx(n - 2)
+            quantise_done(n - 1, 1)
             group_v(n)
-            for piece in range(first_piece, first_piece + W_PER_ROUND):
-                for half in range(2):
-                    turn_w(piece, half)
-                    group_w(piece, half)
-            if n + 1 == len(steps) + 2:
-                project(BLOCKS - 1, range(GROUPS - 1))
-            elif n == len(steps) + 2:
-                project(BLOCKS - 1, [GROUPS - 1])
-                finish(BLOCKS - 1)
-            elif n in project_in_round:
-                project(project_in_round[n], range(GROUPS))
-                finish(project_in_round[n])
+            exponentials(n, 3)
+            group_half(halves[1])
+            turn_q_and_k(n + QK_LEAD + 1, 0)
+            project(*chunk_of(n + 1, 0), ALL)
+            group_half(halves[2])
+
+        n = len(steps)
+        before, last = BLOCK_ORDER[-2:]
+        turn_e(n - 1, 0)
+        turn_e(n - 1, 1)
+        quantise_e(n - 2)
+        quantise_ctx(n - 3)
+        invert_rowsums(n - 2)
+        invert_rowsums(n - 1)
+        group_e(n - 1, 0)
+        group_e(n - 1, 1)
+        first_product(n - 2)
+        project(before, 0, ALL)
+        normalise(n - 2)
+        turn_ctx(n - 2)
+        project(before, 1, ALL)
+        add_bias(before, 0)
+        scale_and_store(before, 0, nc.gpsimd)
+        quantise_e(n - 1)
+        group_ctx(n - 2)
+        first_product(n - 1)
+        normalise(n - 1)
+        turn_ctx(n - 1)
+        project(before, 2, ALL)
+        quantise_ctx(n - 2)
+        add_bias(before, 1)
+        scale_and_store(before, 1, nc.gpsimd)
+        group_ctx(n - 1)
+        for c in range(CHUNKS):
+            project(last, c, range(GROUPS - 1))
+        add_bias(before, 2)
+        scale_and_store(before, 2, nc.gpsimd)
+        quantise_ctx(n - 1)
+        for c in range(CHUNKS):
+            project(last, c, [GROUPS - 1])
+        add_bias(last, 0)
+        add_bias(last, 1)
+        scale_and_store(last, 0, nc.vector)
+        add_bias(last, 2)
+        scale_and_store(last, 1, nc.vector)
+        scale_and_store(last, 2, nc.vector)

@@ -71,22 +71,29 @@ def tile_onedscaleparallelmha_pb_kernel(tc, q_rot, k_rot, v, feat_mask, wo_w, wo
             cols = slice(groups[0] * GROUP * DH, (groups[-1] + 1) * GROUP * DH)
             nc.sync.dma_start(out=sb[:, i, cols], in_=rows[i][:, cols])
 
+        def load_v(g):
+            cols = slice(g * CHUNK, (g + 1) * CHUNK)
+            v_rows = v.rearrange("b (c p e) h d -> (b c) p e (h d)", c=2, e=2)
+            for c in range(2):
+                nc.sync.dma_start(out=v_sb[:, 2 * c : 2 * c + 2, cols], in_=v_rows[c][:, :, cols])
+
         ALL = range(GROUPS)
         def load_w(c):
             nc.sync.dma_start(out=w_sb[:, 4 * c : 4 * c + 4, :], in_=w_rows[:, 4 * c : 4 * c + 4, :])
 
-        for g in range(GROUPS):
-            load(q_rows, q_sb, 0, [g])
-            load(k_rows, k_sb, 0, [g])
+        load(q_rows, q_sb, 0, [0])
+        load(k_rows, k_sb, 0, [0])
         nc.sync.dma_start(out=vector_rows[0:1, 0, :], in_=feat_mask.unsqueeze(0))
         nc.sync.dma_start(out=vector_rows[0:1, 1, :], in_=wo_b.unsqueeze(0))
-        nc.sync.dma_start(
-            out=v_sb[:].rearrange("p (c e) f -> p c (e f)", c=2),
-            in_=v.rearrange("b (c p e) h d -> p (b c) (e h d)", c=2, e=2),
-        )
+        load_v(0)
+        for g in (1, 2):
+            load(q_rows, q_sb, 0, [g])
+            load(k_rows, k_sb, 0, [g])
+        load_v(1)
         for i in (1, 2, 3):
             load(k_rows, k_sb, i, ALL)
         load(q_rows, q_sb, 3, ALL)
+        load_v(2)
         load_w(0)
         load(q_rows, q_sb, 2, ALL)
         load(q_rows, q_sb, 1, ALL)
@@ -223,13 +230,13 @@ def tile_onedscaleparallelmha_pb_kernel(tc, q_rot, k_rot, v, feat_mask, wo_w, wo
                     first = 256 * g + 128 * u
                     nc.tensor.transpose(w_banks[piece, half][:, u, b, :], w_words[:, first : first + P], ident_f32[:])
 
-        def group_w(piece, half):
+        def group_w(piece, half, move):
             if not 0 <= piece < W_PIECES:
                 return
             if half == 0:
                 w_grouped[piece] = work.tile([P, CHUNK, PACK], BF16, name="w_grouped", tag="grouped", align_bytes=64)
             words = w_grouped[piece][:].rearrange("p o j -> p (o j)").bitcast(F32).rearrange("p (o u) -> p o u", u=2)
-            nc.scalar.copy(
+            move(
                 out=words[:, half * 2 * P : (half + 1) * 2 * P, :],
                 in_=w_banks[piece, half][:].rearrange("p u b o -> p (b o) u"),
             )
@@ -382,7 +389,7 @@ def tile_onedscaleparallelmha_pb_kernel(tc, q_rot, k_rot, v, feat_mask, wo_w, wo
             if not valid(n):
                 return
             ctx_grouped[n] = work.tile([P, P, PACK], BF16, name="ctx_grouped", align_bytes=64)
-            nc.vector.tensor_copy(
+            nc.scalar.copy(
                 out=ctx_grouped[n][:].rearrange("p t a -> p (t a)").bitcast(F32).rearrange("p (t c) -> p t c", c=2),
                 in_=ctx_banks[n][:].rearrange("p c t -> p t c"),
             )
@@ -430,7 +437,7 @@ def tile_onedscaleparallelmha_pb_kernel(tc, q_rot, k_rot, v, feat_mask, wo_w, wo
             engine.tensor_tensor(out=result[:], in0=biased[i, c][:], in1=fm_bc[:, cols], op=ALU.mult)
             nc.sync.dma_start(out=out_rows[i][:, cols], in_=result[:])
 
-        finished = {6: [(0, 0)], 7: [(0, 1)], 9: [(1, 0), (0, 2)], 10: [(1, 1)], 11: [(1, 2)]}
+        finished = {7: [(0, 0)], 8: [(0, 1)], 9: [(0, 2), (1, 0)], 10: [(1, 1)], 11: [(1, 2)], 12: [(2, 0)]}
 
         def chunk_of(n, k):
             found = finished.get(n, [])
@@ -443,7 +450,7 @@ def tile_onedscaleparallelmha_pb_kernel(tc, q_rot, k_rot, v, feat_mask, wo_w, wo
             turn_w(half // 2, half % 2)
 
         def group_half(half):
-            group_w(half // 2, half % 2)
+            group_w(half // 2, half % 2, nc.vector.tensor_copy if half % W_HALVES_PER_ROUND == 1 else nc.scalar.copy)
 
         def quantise_done(n, k):
             done = [half // 2 for half in halves_of(n) if half % 2 == 1]
@@ -452,89 +459,87 @@ def tile_onedscaleparallelmha_pb_kernel(tc, q_rot, k_rot, v, feat_mask, wo_w, wo
 
         for n in range(-QK_LEAD - 1, len(steps)):
             halves = halves_of(n)
-            scores(n + 1, 1)
+            scores(n + 1, 0)
             turn_e(n - 1, 0)
             turn_e(n - 1, 1)
             clear_e(n)
             quantise_e(n - 2)
-            quantise_ctx(n - 3)
             quantise_done(n - 1, 0)
-            quantise_v(n - 1)
-            maxima(n + 1, 0)
+            quantise_done(n - 1, 1)
+            maxima(n, 2)
             invert_rowsums(n - 2)
+            quantise_v(n - 1)
             add_bias(*chunk_of(n, 0))
             exponentials(n, 0)
-            keep_q_and_k(n + QK_LEAD, 0)
-            scale_and_store(*chunk_of(n, 0), nc.gpsimd)
-
+            keep_q_and_k(n + 2, 0)
+            maxima(n, 3)
             first_product(n - 2)
+            scores(n + 1, 1)
             project(*chunk_of(n, 1), ALL)
-            scores(n + 1, 2)
-            turn_q_and_k(n + QK_LEAD, 1)
-            maxima(n + 1, 1)
+            turn_q_and_k(n + 2, 1)
             normalise(n - 2)
             exponentials(n, 1)
             group_e(n - 1, 0)
-
+            scale_and_store(*chunk_of(n, 0), nc.gpsimd)
             turn_half(halves[0])
-            scores(n + 1, 3)
+            scores(n + 1, 2)
             exponentials(n, 2)
             group_e(n - 1, 1)
-            keep_q_and_k(n + QK_LEAD, 1)
+            keep_q_and_k(n + 2, 1)
             turn_ctx(n - 2)
-            maxima(n + 1, 2)
+            quantise_ctx(n - 3)
             add_bias(*chunk_of(n, 1))
-            scale_and_store(*chunk_of(n, 1), nc.gpsimd)
+            maxima(n + 1, 0)
             group_half(halves[0])
-
             turn_half(halves[1])
             spread_over_partitions(n)
-            scores(n + 2, 0)
+            scores(n + 1, 3)
             turn_half(halves[2])
-            maxima(n + 1, 3)
-            group_ctx(n - 2)
-            quantise_done(n - 1, 1)
+            maxima(n + 1, 1)
             group_v(n)
             exponentials(n, 3)
+            group_ctx(n - 2)
             group_half(halves[1])
-            turn_q_and_k(n + QK_LEAD + 1, 0)
+            turn_q_and_k(n + 3, 0)
             project(*chunk_of(n + 1, 0), ALL)
+            scale_and_store(*chunk_of(n, 1), nc.gpsimd)
             group_half(halves[2])
 
         n = len(steps)
         before, last = BLOCK_ORDER[-2:]
         turn_e(n - 1, 0)
         turn_e(n - 1, 1)
+        add_bias(before, 0)
         quantise_e(n - 2)
         quantise_ctx(n - 3)
         invert_rowsums(n - 2)
         invert_rowsums(n - 1)
         group_e(n - 1, 0)
         group_e(n - 1, 1)
+        scale_and_store(before, 0, nc.vector)
         first_product(n - 2)
-        project(before, 0, ALL)
+        project(before, 1, ALL)
         normalise(n - 2)
         turn_ctx(n - 2)
-        project(before, 1, ALL)
-        add_bias(before, 0)
-        scale_and_store(before, 0, nc.gpsimd)
         quantise_e(n - 1)
         group_ctx(n - 2)
         first_product(n - 1)
+        add_bias(before, 1)
+        project(before, 2, ALL)
         normalise(n - 1)
         turn_ctx(n - 1)
-        project(before, 2, ALL)
         quantise_ctx(n - 2)
-        add_bias(before, 1)
-        scale_and_store(before, 1, nc.gpsimd)
+        scale_and_store(before, 1, nc.vector)
         group_ctx(n - 1)
-        for c in range(CHUNKS):
-            project(last, c, range(GROUPS - 1))
         add_bias(before, 2)
-        scale_and_store(before, 2, nc.gpsimd)
+        project(last, 0, range(2))
+        project(last, 1, range(2))
+        project(last, 2, range(2))
         quantise_ctx(n - 1)
-        for c in range(CHUNKS):
-            project(last, c, [GROUPS - 1])
+        scale_and_store(before, 2, nc.vector)
+        project(last, 0, [2])
+        project(last, 1, [2])
+        project(last, 2, [2])
         add_bias(last, 0)
         add_bias(last, 1)
         scale_and_store(last, 0, nc.vector)

@@ -35,6 +35,8 @@ W_PIECES = GROUPS * CHUNKS
 W_HALVES_PER_ROUND = 3
 W_FIRST_ROUND = 2
 V_ON_SCALAR = ()
+TURNED_BY_PRODUCT = range(2, 7)
+KEPT_BY_VECTOR = range(2)
 QK_LEAD = 2
 BLOCK_ORDER = (0, 3, 2, 1)
 QK_UNITS = {0: (((0, 0), (1, 0)),), 3: (((1, 1), (1, 2)), ((0, 3), (1, 3))), 2: (((0, 1), (0, 2)),), 1: ()}
@@ -71,29 +73,22 @@ def tile_onedscaleparallelmha_pb_kernel(tc, q_rot, k_rot, v, feat_mask, wo_w, wo
             cols = slice(groups[0] * GROUP * DH, (groups[-1] + 1) * GROUP * DH)
             nc.sync.dma_start(out=sb[:, i, cols], in_=rows[i][:, cols])
 
-        def load_v(g):
-            cols = slice(g * CHUNK, (g + 1) * CHUNK)
-            v_rows = v.rearrange("b (c p e) h d -> (b c) p e (h d)", c=2, e=2)
-            for c in range(2):
-                nc.sync.dma_start(out=v_sb[:, 2 * c : 2 * c + 2, cols], in_=v_rows[c][:, :, cols])
-
         ALL = range(GROUPS)
         def load_w(c):
             nc.sync.dma_start(out=w_sb[:, 4 * c : 4 * c + 4, :], in_=w_rows[:, 4 * c : 4 * c + 4, :])
 
-        load(q_rows, q_sb, 0, [0])
-        load(k_rows, k_sb, 0, [0])
-        nc.sync.dma_start(out=vector_rows[0:1, 0, :], in_=feat_mask.unsqueeze(0))
-        nc.sync.dma_start(out=vector_rows[0:1, 1, :], in_=wo_b.unsqueeze(0))
-        load_v(0)
-        for g in (1, 2):
+        for g in range(GROUPS):
             load(q_rows, q_sb, 0, [g])
             load(k_rows, k_sb, 0, [g])
-        load_v(1)
+        nc.sync.dma_start(out=vector_rows[0:1, 0, :], in_=feat_mask.unsqueeze(0))
+        nc.sync.dma_start(out=vector_rows[0:1, 1, :], in_=wo_b.unsqueeze(0))
+        nc.sync.dma_start(
+            out=v_sb[:].rearrange("p (c e) f -> p c (e f)", c=2),
+            in_=v.rearrange("b (c p e) h d -> p (b c) (e h d)", c=2, e=2),
+        )
         for i in (1, 2, 3):
             load(k_rows, k_sb, i, ALL)
         load(q_rows, q_sb, 3, ALL)
-        load_v(2)
         load_w(0)
         load(q_rows, q_sb, 2, ALL)
         load(q_rows, q_sb, 1, ALL)
@@ -187,7 +182,12 @@ def tile_onedscaleparallelmha_pb_kernel(tc, q_rot, k_rot, v, feat_mask, wo_w, wo
                 rows = (q_sb, k_sb)[side]
                 for j in range(GROUP):
                     h = g * GROUP + j
-                    nc.tensor.transpose(qk_banks[n, u][:, slot, j, :], rows[:, i, h * DH : (h + 1) * DH], ident_bf[:])
+                    turned = qk_banks[n, u][:, slot, j, :]
+                    block = rows[:, i, h * DH : (h + 1) * DH]
+                    if u == 0 and n in TURNED_BY_PRODUCT:
+                        nc.tensor.matmul(out=turned, lhsT=block, rhs=ident_bf[:], start=True, stop=True)
+                    else:
+                        nc.tensor.transpose(turned, block, ident_bf[:])
 
         def keep_q_and_k(n, u):
             if u >= len(qk_units(n)):
@@ -199,7 +199,8 @@ def tile_onedscaleparallelmha_pb_kernel(tc, q_rot, k_rot, v, feat_mask, wo_w, wo
                 dst = qk_t[:, side, heads, i * P : (i + 2) * P].rearrange("p h (b t) -> p b h t", b=2)
             else:
                 dst = qk_t[:, :, heads, i * P : (i + 1) * P]
-            nc.scalar.copy(out=dst, in_=qk_banks[n, u][:])
+            move = nc.vector.tensor_copy if n in KEPT_BY_VECTOR else nc.scalar.copy
+            move(out=dst, in_=qk_banks[n, u][:])
 
         def group_v(g):
             if not 0 <= g < GROUPS:
@@ -437,7 +438,7 @@ def tile_onedscaleparallelmha_pb_kernel(tc, q_rot, k_rot, v, feat_mask, wo_w, wo
             engine.tensor_tensor(out=result[:], in0=biased[i, c][:], in1=fm_bc[:, cols], op=ALU.mult)
             nc.sync.dma_start(out=out_rows[i][:, cols], in_=result[:])
 
-        finished = {7: [(0, 0)], 8: [(0, 1)], 9: [(0, 2), (1, 0)], 10: [(1, 1)], 11: [(1, 2)], 12: [(2, 0)]}
+        finished = {6: [(0, 0)], 7: [(0, 1)], 9: [(0, 2), (1, 0)], 10: [(1, 1)], 11: [(1, 2)], 12: [(2, 0)]}
 
         def chunk_of(n, k):
             found = finished.get(n, [])
@@ -450,7 +451,7 @@ def tile_onedscaleparallelmha_pb_kernel(tc, q_rot, k_rot, v, feat_mask, wo_w, wo
             turn_w(half // 2, half % 2)
 
         def group_half(half):
-            group_w(half // 2, half % 2, nc.vector.tensor_copy if half % W_HALVES_PER_ROUND == 1 else nc.scalar.copy)
+            group_w(half // 2, half % 2, nc.vector.tensor_copy if half in (1, 4, 7) else nc.scalar.copy)
 
         def quantise_done(n, k):
             done = [half // 2 for half in halves_of(n) if half % 2 == 1]
@@ -459,79 +460,79 @@ def tile_onedscaleparallelmha_pb_kernel(tc, q_rot, k_rot, v, feat_mask, wo_w, wo
 
         for n in range(-QK_LEAD - 1, len(steps)):
             halves = halves_of(n)
-            scores(n + 1, 0)
             turn_e(n - 1, 0)
-            turn_e(n - 1, 1)
             clear_e(n)
+            invert_rowsums(n - 2)
             quantise_e(n - 2)
+            maxima(n, 2)
+            quantise_ctx(n - 3)
             quantise_done(n - 1, 0)
             quantise_done(n - 1, 1)
-            maxima(n, 2)
-            invert_rowsums(n - 2)
-            quantise_v(n - 1)
             add_bias(*chunk_of(n, 0))
-            exponentials(n, 0)
-            keep_q_and_k(n + 2, 0)
-            maxima(n, 3)
             first_product(n - 2)
-            scores(n + 1, 1)
             project(*chunk_of(n, 1), ALL)
-            turn_q_and_k(n + 2, 1)
-            normalise(n - 2)
-            exponentials(n, 1)
+            scores(n + 1, 0)
+            keep_q_and_k(n + 2, 0)
             group_e(n - 1, 0)
-            scale_and_store(*chunk_of(n, 0), nc.gpsimd)
-            turn_half(halves[0])
-            scores(n + 1, 2)
             exponentials(n, 2)
+            turn_e(n - 1, 1)
+            turn_q_and_k(n + 2, 1)
+            turn_half(halves[0])
+            scores(n + 1, 1)
+            normalise(n - 2)
+            maxima(n, 3)
+            scale_and_store(*chunk_of(n, 0), nc.gpsimd)
+            group_v(n)
             group_e(n - 1, 1)
             keep_q_and_k(n + 2, 1)
-            turn_ctx(n - 2)
-            quantise_ctx(n - 3)
-            add_bias(*chunk_of(n, 1))
-            maxima(n + 1, 0)
             group_half(halves[0])
+            exponentials(n, 3)
+            turn_ctx(n - 2)
+            scores(n + 1, 2)
             turn_half(halves[1])
             spread_over_partitions(n)
-            scores(n + 1, 3)
-            turn_half(halves[2])
-            maxima(n + 1, 1)
-            group_v(n)
-            exponentials(n, 3)
+            add_bias(*chunk_of(n, 1))
+            scale_and_store(*chunk_of(n, 1), nc.gpsimd)
+            maxima(n + 1, 0)
+            quantise_v(n - 1)
             group_ctx(n - 2)
             group_half(halves[1])
-            turn_q_and_k(n + 3, 0)
+            exponentials(n + 1, 0)
             project(*chunk_of(n + 1, 0), ALL)
-            scale_and_store(*chunk_of(n, 1), nc.gpsimd)
+            turn_half(halves[2])
+            scores(n + 1, 3)
+            turn_q_and_k(n + 3, 0)
+            maxima(n + 1, 1)
             group_half(halves[2])
+            exponentials(n + 1, 1)
 
         n = len(steps)
         before, last = BLOCK_ORDER[-2:]
         turn_e(n - 1, 0)
         turn_e(n - 1, 1)
-        add_bias(before, 0)
-        quantise_e(n - 2)
-        quantise_ctx(n - 3)
         invert_rowsums(n - 2)
         invert_rowsums(n - 1)
+        quantise_e(n - 2)
+        add_bias(before, 0)
         group_e(n - 1, 0)
         group_e(n - 1, 1)
-        scale_and_store(before, 0, nc.vector)
         first_product(n - 2)
         project(before, 1, ALL)
+        quantise_ctx(n - 3)
         normalise(n - 2)
+        scale_and_store(before, 0, nc.vector)
         turn_ctx(n - 2)
         quantise_e(n - 1)
-        group_ctx(n - 2)
         first_product(n - 1)
         add_bias(before, 1)
+        group_ctx(n - 2)
         project(before, 2, ALL)
         normalise(n - 1)
         turn_ctx(n - 1)
         quantise_ctx(n - 2)
+        add_bias(before, 2)
         scale_and_store(before, 1, nc.vector)
         group_ctx(n - 1)
-        add_bias(before, 2)
         project(last, 0, range(2))
         project(last, 1, range(2))
         project(last, 2, range(2))

@@ -34,8 +34,7 @@ FLOPS = 2 * H * S * S * DH * 2 + 2 * S * E * E
 W_PIECES = GROUPS * CHUNKS
 W_HALVES_PER_ROUND = 3
 W_FIRST_ROUND = 2
-V_ON_SCALAR = ()
-TURNED_BY_PRODUCT = range(2, 7)
+TURNED_BY_PRODUCT = range(2, 9)
 KEPT_BY_VECTOR = range(2)
 QK_LEAD = 2
 BLOCK_ORDER = (0, 3, 2, 1)
@@ -66,8 +65,10 @@ def tile_onedscaleparallelmha_pb_kernel(tc, q_rot, k_rot, v, feat_mask, wo_w, wo
         k_sb = keep.tile([P, BLOCKS, E], BF16)
         v_sb = keep.tile([P, PACK, E], BF16)
         w_sb = keep.tile([P, H, E], BF16)
-        vector_rows = const.tile([P, 2, E], BF16)
-        nc.vector.memset(vector_rows[:].rearrange("p k f -> p (k f)").bitcast(I32), 0)
+        fm_row = const.tile([P, E], BF16)
+        nc.vector.memset(fm_row[:].bitcast(I32), 0)
+        fm_bc = const.tile([P, E], BF16)
+        b_bc = const.tile([P, E], BF16)
 
         def load(rows, sb, i, groups):
             cols = slice(groups[0] * GROUP * DH, (groups[-1] + 1) * GROUP * DH)
@@ -80,8 +81,7 @@ def tile_onedscaleparallelmha_pb_kernel(tc, q_rot, k_rot, v, feat_mask, wo_w, wo
         for g in range(GROUPS):
             load(q_rows, q_sb, 0, [g])
             load(k_rows, k_sb, 0, [g])
-        nc.sync.dma_start(out=vector_rows[0:1, 0, :], in_=feat_mask.unsqueeze(0))
-        nc.sync.dma_start(out=vector_rows[0:1, 1, :], in_=wo_b.unsqueeze(0))
+        nc.sync.dma_start(out=fm_row[0:1, :], in_=feat_mask.unsqueeze(0))
         nc.sync.dma_start(
             out=v_sb[:].rearrange("p (c e) f -> p c (e f)", c=2),
             in_=v.rearrange("b (c p e) h d -> p (b c) (e h d)", c=2, e=2),
@@ -94,6 +94,7 @@ def tile_onedscaleparallelmha_pb_kernel(tc, q_rot, k_rot, v, feat_mask, wo_w, wo
         load(q_rows, q_sb, 1, ALL)
         load_w(1)
         load_w(2)
+        nc.sync.dma_start(out=b_bc[:], in_=wo_b.partition_broadcast(P))
 
         e_sb = keep.tile([P, 2 * GROUP, S], BF16)
         nc.vector.memset(e_sb[:].rearrange("p r u -> p (r u)").bitcast(I32), 0)
@@ -116,9 +117,6 @@ def tile_onedscaleparallelmha_pb_kernel(tc, q_rot, k_rot, v, feat_mask, wo_w, wo
         nc.vector.tensor_copy(out=mask_bf[:], in_=mask_f32[:])
         ones_bf = const.tile([P, P], BF16)
         nc.vector.memset(ones_bf[:], 1.0)
-        repeated_rows = const.tile([P, 2 * E], BF16)
-        fm_bc = repeated_rows[:, :E]
-        b_bc = repeated_rows[:, E:]
 
         qk_t = keep.tile([P, 2, H, S], BF16)
         q_t = qk_t[:, 0]
@@ -155,20 +153,20 @@ def tile_onedscaleparallelmha_pb_kernel(tc, q_rot, k_rot, v, feat_mask, wo_w, wo
 
 
         def spread_over_partitions(k):
-            if not 0 <= k < 2 * E // (2 * CHUNK):
+            first = 2 * k * CHUNK
+            width = min(2 * CHUNK, E - first)
+            if k < 0 or width <= 0:
                 return
-            rows = vector_rows[:].rearrange("p k f -> p (k f)")
-            repeated = ps_scores.tile([P, 2 * CHUNK], BF16, tag="bank")
-            for half in range(2):
-                first = (2 * k + half) * CHUNK
+            repeated = ps_scores.tile([P, width], BF16, name="repeated", tag="bank")
+            for at in range(0, width, CHUNK):
                 nc.tensor.matmul(
-                    out=repeated[:, half * CHUNK : (half + 1) * CHUNK],
+                    out=repeated[:, at : at + CHUNK],
                     lhsT=ones_bf[:],
-                    rhs=rows[:, first : first + CHUNK],
+                    rhs=fm_row[:, first + at : first + at + CHUNK],
                     start=True,
                     stop=True,
                 )
-            nc.scalar.copy(out=repeated_rows[:, 2 * k * CHUNK : 2 * (k + 1) * CHUNK], in_=repeated[:])
+            nc.scalar.copy(out=fm_bc[:, first : first + width], in_=repeated[:])
 
         def qk_units(n):
             return QK_UNITS[steps[n][0]] if valid(n) else ()
@@ -205,10 +203,15 @@ def tile_onedscaleparallelmha_pb_kernel(tc, q_rot, k_rot, v, feat_mask, wo_w, wo
         def group_v(g):
             if not 0 <= g < GROUPS:
                 return
-            move = nc.scalar.copy if g in V_ON_SCALAR else nc.vector.tensor_copy
             cols = slice(g * CHUNK, (g + 1) * CHUNK)
+            rows = v_sb[:, :, cols].rearrange("p a f -> p f a")
             v_grouped[g] = work.tile([P, CHUNK, PACK], BF16, name="v_grouped", tag="v_grouped", bufs=2, align_bytes=64)
-            move(out=v_grouped[g][:], in_=v_sb[:, :, cols].rearrange("p a f -> p f a"))
+            if g == 0:
+                nc.vector.tensor_copy(out=v_grouped[g][:], in_=rows)
+            else:
+                nc.gpsimd.tensor_scalar(
+                    out=v_grouped[g][:], in0=rows, scalar1=1.0, scalar2=0.0, op0=ALU.mult, op1=ALU.add
+                )
 
         def quantise_v(g):
             if not 0 <= g < GROUPS:
@@ -425,7 +428,7 @@ def tile_onedscaleparallelmha_pb_kernel(tc, q_rot, k_rot, v, feat_mask, wo_w, wo
         def add_bias(i, c):
             if not 0 <= i < BLOCKS:
                 return
-            biased[i, c] = work.tile([P, CHUNK], F32, name="biased")
+            biased[i, c] = work.tile([P, CHUNK], F32, name="biased", bufs=4)
             nc.vector.tensor_tensor(
                 out=biased[i, c][:], in0=out_banks[i, c][:], in1=b_bc[:, c * CHUNK : (c + 1) * CHUNK], op=ALU.add
             )
@@ -434,7 +437,7 @@ def tile_onedscaleparallelmha_pb_kernel(tc, q_rot, k_rot, v, feat_mask, wo_w, wo
             if not 0 <= i < BLOCKS:
                 return
             cols = slice(c * CHUNK, (c + 1) * CHUNK)
-            result = work.tile([P, CHUNK], F32, name="result")
+            result = work.tile([P, CHUNK], F32, name="result", bufs=6)
             engine.tensor_tensor(out=result[:], in0=biased[i, c][:], in1=fm_bc[:, cols], op=ALU.mult)
             nc.sync.dma_start(out=out_rows[i][:, cols], in_=result[:])
 
@@ -460,11 +463,11 @@ def tile_onedscaleparallelmha_pb_kernel(tc, q_rot, k_rot, v, feat_mask, wo_w, wo
 
         for n in range(-QK_LEAD - 1, len(steps)):
             halves = halves_of(n)
-            turn_e(n - 1, 0)
+            turn_e(n - 1, 1)
             clear_e(n)
+            maxima(n, 2)
             invert_rowsums(n - 2)
             quantise_e(n - 2)
-            maxima(n, 2)
             quantise_ctx(n - 3)
             quantise_done(n - 1, 0)
             quantise_done(n - 1, 1)
@@ -473,57 +476,55 @@ def tile_onedscaleparallelmha_pb_kernel(tc, q_rot, k_rot, v, feat_mask, wo_w, wo
             project(*chunk_of(n, 1), ALL)
             scores(n + 1, 0)
             keep_q_and_k(n + 2, 0)
-            group_e(n - 1, 0)
+            group_e(n - 1, 1)
             exponentials(n, 2)
-            turn_e(n - 1, 1)
             turn_q_and_k(n + 2, 1)
             turn_half(halves[0])
             scores(n + 1, 1)
+            spread_over_partitions(n)
             normalise(n - 2)
             maxima(n, 3)
             scale_and_store(*chunk_of(n, 0), nc.gpsimd)
             group_v(n)
-            group_e(n - 1, 1)
             keep_q_and_k(n + 2, 1)
             group_half(halves[0])
             exponentials(n, 3)
+            turn_half(halves[1])
             turn_ctx(n - 2)
             scores(n + 1, 2)
-            turn_half(halves[1])
-            spread_over_partitions(n)
             add_bias(*chunk_of(n, 1))
             scale_and_store(*chunk_of(n, 1), nc.gpsimd)
             maxima(n + 1, 0)
             quantise_v(n - 1)
-            group_ctx(n - 2)
             group_half(halves[1])
+            group_ctx(n - 2)
             exponentials(n + 1, 0)
+            turn_e(n, 0)
             project(*chunk_of(n + 1, 0), ALL)
             turn_half(halves[2])
             scores(n + 1, 3)
-            turn_q_and_k(n + 3, 0)
             maxima(n + 1, 1)
+            group_e(n, 0)
+            turn_q_and_k(n + 3, 0)
             group_half(halves[2])
             exponentials(n + 1, 1)
 
         n = len(steps)
         before, last = BLOCK_ORDER[-2:]
-        turn_e(n - 1, 0)
         turn_e(n - 1, 1)
         invert_rowsums(n - 2)
         invert_rowsums(n - 1)
         quantise_e(n - 2)
+        quantise_ctx(n - 3)
         add_bias(before, 0)
-        group_e(n - 1, 0)
         group_e(n - 1, 1)
         first_product(n - 2)
         project(before, 1, ALL)
-        quantise_ctx(n - 3)
         normalise(n - 2)
-        scale_and_store(before, 0, nc.vector)
         turn_ctx(n - 2)
         quantise_e(n - 1)
         first_product(n - 1)
+        scale_and_store(before, 0, nc.vector)
         add_bias(before, 1)
         group_ctx(n - 2)
         project(before, 2, ALL)
@@ -535,15 +536,15 @@ def tile_onedscaleparallelmha_pb_kernel(tc, q_rot, k_rot, v, feat_mask, wo_w, wo
         group_ctx(n - 1)
         project(last, 0, range(2))
         project(last, 1, range(2))
-        project(last, 2, range(2))
         quantise_ctx(n - 1)
         scale_and_store(before, 2, nc.vector)
         project(last, 0, [2])
-        project(last, 1, [2])
-        project(last, 2, [2])
         add_bias(last, 0)
+        project(last, 1, [2])
         add_bias(last, 1)
+        project(last, 2, range(2))
         scale_and_store(last, 0, nc.vector)
+        project(last, 2, [2])
         add_bias(last, 2)
         scale_and_store(last, 1, nc.vector)
         scale_and_store(last, 2, nc.vector)

@@ -206,12 +206,7 @@ def tile_onedscaleparallelmha_pb_kernel(tc, q_rot, k_rot, v, feat_mask, wo_w, wo
             cols = slice(g * CHUNK, (g + 1) * CHUNK)
             rows = v_sb[:, :, cols].rearrange("p a f -> p f a")
             v_grouped[g] = work.tile([P, CHUNK, PACK], BF16, name="v_grouped", tag="v_grouped", bufs=2, align_bytes=64)
-            if g == 0:
-                nc.vector.tensor_copy(out=v_grouped[g][:], in_=rows)
-            else:
-                nc.gpsimd.tensor_scalar(
-                    out=v_grouped[g][:], in0=rows, scalar1=1.0, scalar2=0.0, op0=ALU.mult, op1=ALU.add
-                )
+            nc.vector.tensor_copy(out=v_grouped[g][:], in_=rows)
 
         def quantise_v(g):
             if not 0 <= g < GROUPS:

@@ -70,28 +70,27 @@ def tile_onedscaleparallelmha_pb_kernel(tc, q_rot, k_rot, v, feat_mask, wo_w, wo
         fm_bc = const.tile([P, E], BF16)
         b_bc = const.tile([P, E], BF16)
 
-        def load(rows, sb, i, groups):
-            cols = slice(groups[0] * GROUP * DH, (groups[-1] + 1) * GROUP * DH)
-            nc.sync.dma_start(out=sb[:, i, cols], in_=rows[i][:, cols])
+        def load(rows, sb, i):
+            nc.sync.dma_start(out=sb[:, i, :], in_=rows[i])
 
         ALL = range(GROUPS)
+
         def load_w(c):
             nc.sync.dma_start(out=w_sb[:, 4 * c : 4 * c + 4, :], in_=w_rows[:, 4 * c : 4 * c + 4, :])
 
-        for g in range(GROUPS):
-            load(q_rows, q_sb, 0, [g])
-            load(k_rows, k_sb, 0, [g])
+        load(q_rows, q_sb, 0)
+        load(k_rows, k_sb, 0)
         nc.sync.dma_start(out=fm_row[0:1, :], in_=feat_mask.unsqueeze(0))
         nc.sync.dma_start(
             out=v_sb[:].rearrange("p (c e) f -> p c (e f)", c=2),
             in_=v.rearrange("b (c p e) h d -> p (b c) (e h d)", c=2, e=2),
         )
         for i in (1, 2, 3):
-            load(k_rows, k_sb, i, ALL)
-        load(q_rows, q_sb, 3, ALL)
+            load(k_rows, k_sb, i)
+        load(q_rows, q_sb, 3)
         load_w(0)
-        load(q_rows, q_sb, 2, ALL)
-        load(q_rows, q_sb, 1, ALL)
+        load(q_rows, q_sb, 2)
+        load(q_rows, q_sb, 1)
         load_w(1)
         load_w(2)
         nc.sync.dma_start(out=b_bc[:], in_=wo_b.partition_broadcast(P))
@@ -229,13 +228,13 @@ def tile_onedscaleparallelmha_pb_kernel(tc, q_rot, k_rot, v, feat_mask, wo_w, wo
                     first = 256 * g + 128 * u
                     nc.tensor.transpose(w_banks[piece, half][:, u, b, :], w_words[:, first : first + P], ident_f32[:])
 
-        def group_w(piece, half, move):
+        def group_w(piece, half):
             if not 0 <= piece < W_PIECES:
                 return
             if half == 0:
                 w_grouped[piece] = work.tile([P, CHUNK, PACK], BF16, name="w_grouped", tag="grouped", align_bytes=64)
             words = w_grouped[piece][:].rearrange("p o j -> p (o j)").bitcast(F32).rearrange("p (o u) -> p o u", u=2)
-            move(
+            nc.scalar.copy(
                 out=words[:, half * 2 * P : (half + 1) * 2 * P, :],
                 in_=w_banks[piece, half][:].rearrange("p u b o -> p (b o) u"),
             )
@@ -449,7 +448,7 @@ def tile_onedscaleparallelmha_pb_kernel(tc, q_rot, k_rot, v, feat_mask, wo_w, wo
             turn_w(half // 2, half % 2)
 
         def group_half(half):
-            group_w(half // 2, half % 2, nc.vector.tensor_copy if half in (1, 4, 7) else nc.scalar.copy)
+            group_w(half // 2, half % 2)
 
         def quantise_done(n, k):
             done = [half // 2 for half in halves_of(n) if half % 2 == 1]
@@ -473,10 +472,10 @@ def tile_onedscaleparallelmha_pb_kernel(tc, q_rot, k_rot, v, feat_mask, wo_w, wo
             keep_q_and_k(n + 2, 0)
             group_e(n - 1, 1)
             exponentials(n, 2)
+            spread_over_partitions(n)
             turn_q_and_k(n + 2, 1)
             turn_half(halves[0])
             scores(n + 1, 1)
-            spread_over_partitions(n)
             normalise(n - 2)
             maxima(n, 3)
             scale_and_store(*chunk_of(n, 0), nc.gpsimd)

@@ -34,16 +34,13 @@ FLOPS = 2 * H * S * S * DH * 2 + 2 * S * E * E
 W_PIECES = GROUPS * CHUNKS
 W_HALVES_PER_ROUND = 3
 W_FIRST_ROUND = 2
-TURNED_BY_PRODUCT = range(2, 9)
 KEPT_BY_VECTOR = range(2)
 QK_LEAD = 2
-BLOCK_ORDER = (0, 3, 2, 1)
-QK_UNITS = {0: (((0, 0), (1, 0)),), 3: (((1, 1), (1, 2)), ((0, 3), (1, 3))), 2: (((0, 1), (0, 2)),), 1: ()}
 
 
 def tile_onedscaleparallelmha_pb_kernel(tc, q_rot, k_rot, v, feat_mask, wo_w, wo_b, out):
     nc = tc.nc
-    steps = [(i, g) for i in BLOCK_ORDER for g in range(GROUPS)]
+    steps = [(i, g) for i in range(BLOCKS) for g in range(GROUPS)]
 
     def valid(n):
         return 0 <= n < len(steps)
@@ -78,21 +75,23 @@ def tile_onedscaleparallelmha_pb_kernel(tc, q_rot, k_rot, v, feat_mask, wo_w, wo
         def load_w(c):
             nc.sync.dma_start(out=w_sb[:, 4 * c : 4 * c + 4, :], in_=w_rows[:, 4 * c : 4 * c + 4, :])
 
-        load(q_rows, q_sb, 0)
-        load(k_rows, k_sb, 0)
+        for cols in (slice(0, GROUP * DH), slice(GROUP * DH, E)):
+            nc.sync.dma_start(out=q_sb[:, 0, cols], in_=q_rows[0][:, cols])
+            nc.sync.dma_start(out=k_sb[:, 0, cols], in_=k_rows[0][:, cols])
         nc.sync.dma_start(out=fm_row[0:1, :], in_=feat_mask.unsqueeze(0))
         nc.sync.dma_start(
             out=v_sb[:].rearrange("p (c e) f -> p c (e f)", c=2),
             in_=v.rearrange("b (c p e) h d -> p (b c) (e h d)", c=2, e=2),
         )
-        for i in (1, 2, 3):
-            load(k_rows, k_sb, i)
-        load(q_rows, q_sb, 3)
+        load(q_rows, q_sb, 1)
+        load(k_rows, k_sb, 1)
         load_w(0)
         load(q_rows, q_sb, 2)
-        load(q_rows, q_sb, 1)
+        load(k_rows, k_sb, 2)
         load_w(1)
         load_w(2)
+        load(q_rows, q_sb, 3)
+        load(k_rows, k_sb, 3)
         nc.sync.dma_start(out=b_bc[:], in_=wo_b.partition_broadcast(P))
 
         e_sb = keep.tile([P, 2 * GROUP, S], BF16)
@@ -167,37 +166,22 @@ def tile_onedscaleparallelmha_pb_kernel(tc, q_rot, k_rot, v, feat_mask, wo_w, wo
                 )
             nc.scalar.copy(out=fm_bc[:, first : first + width], in_=repeated[:])
 
-        def qk_units(n):
-            return QK_UNITS[steps[n][0]] if valid(n) else ()
-
-        def turn_q_and_k(n, u):
-            if u >= len(qk_units(n)):
+        def turn_q_and_k(n):
+            if not valid(n):
                 return
-            g = steps[n][1]
-            qk_banks[n, u] = ps_turn.tile([P, 2, GROUP, P], BF16, name="qk_bank", tag="turn")
-            for slot, (side, i) in enumerate(qk_units(n)[u]):
-                rows = (q_sb, k_sb)[side]
+            i, g = steps[n]
+            qk_banks[n] = ps_turn.tile([P, 2, GROUP, P], BF16, name="qk_bank", tag="turn")
+            for side, rows in enumerate((q_sb, k_sb)):
                 for j in range(GROUP):
                     h = g * GROUP + j
-                    turned = qk_banks[n, u][:, slot, j, :]
-                    block = rows[:, i, h * DH : (h + 1) * DH]
-                    if u == 0 and n in TURNED_BY_PRODUCT:
-                        nc.tensor.matmul(out=turned, lhsT=block, rhs=ident_bf[:], start=True, stop=True)
-                    else:
-                        nc.tensor.transpose(turned, block, ident_bf[:])
+                    nc.tensor.transpose(qk_banks[n][:, side, j, :], rows[:, i, h * DH : (h + 1) * DH], ident_bf[:])
 
-        def keep_q_and_k(n, u):
-            if u >= len(qk_units(n)):
+        def keep_q_and_k(n):
+            if not valid(n):
                 return
-            g = steps[n][1]
-            heads = slice(g * GROUP, (g + 1) * GROUP)
-            (side, i), (other, i2) = qk_units(n)[u]
-            if side == other:
-                dst = qk_t[:, side, heads, i * P : (i + 2) * P].rearrange("p h (b t) -> p b h t", b=2)
-            else:
-                dst = qk_t[:, :, heads, i * P : (i + 1) * P]
+            i, g = steps[n]
             move = nc.vector.tensor_copy if n in KEPT_BY_VECTOR else nc.scalar.copy
-            move(out=dst, in_=qk_banks[n, u][:])
+            move(out=qk_t[:, :, g * GROUP : (g + 1) * GROUP, i * P : (i + 1) * P], in_=qk_banks[n][:])
 
         def group_v(g):
             if not 0 <= g < GROUPS:
@@ -228,13 +212,13 @@ def tile_onedscaleparallelmha_pb_kernel(tc, q_rot, k_rot, v, feat_mask, wo_w, wo
                     first = 256 * g + 128 * u
                     nc.tensor.transpose(w_banks[piece, half][:, u, b, :], w_words[:, first : first + P], ident_f32[:])
 
-        def group_w(piece, half):
+        def group_w(piece, half, move):
             if not 0 <= piece < W_PIECES:
                 return
             if half == 0:
                 w_grouped[piece] = work.tile([P, CHUNK, PACK], BF16, name="w_grouped", tag="grouped", align_bytes=64)
             words = w_grouped[piece][:].rearrange("p o j -> p (o j)").bitcast(F32).rearrange("p (o u) -> p o u", u=2)
-            nc.scalar.copy(
+            move(
                 out=words[:, half * 2 * P : (half + 1) * 2 * P, :],
                 in_=w_banks[piece, half][:].rearrange("p u b o -> p (b o) u"),
             )
@@ -294,14 +278,6 @@ def tile_onedscaleparallelmha_pb_kernel(tc, q_rot, k_rot, v, feat_mask, wo_w, wo
                 scale=-1.0,
                 accum_out=rowsums[n][:, j : j + 1],
             )
-
-        def clear_e(n):
-            if not valid(n) or not valid(n - 2):
-                return
-            i, before = steps[n][0], steps[n - 2][0]
-            if before > i:
-                rows = slice(e_row(n, 0), e_row(n, 0) + GROUP)
-                nc.gpsimd.memset(e_sb[:, rows, (i + 1) * P : (before + 1) * P].bitcast(I32), 0)
 
         def turn_e(n, pair):
             if not valid(n):
@@ -439,7 +415,7 @@ def tile_onedscaleparallelmha_pb_kernel(tc, q_rot, k_rot, v, feat_mask, wo_w, wo
 
         def chunk_of(n, k):
             found = finished.get(n, [])
-            return (BLOCK_ORDER[found[k][0]], found[k][1]) if k < len(found) else (-1, 0)
+            return found[k] if k < len(found) else (-1, 0)
 
         def halves_of(n):
             return range((n - W_FIRST_ROUND) * W_HALVES_PER_ROUND, (n - W_FIRST_ROUND + 1) * W_HALVES_PER_ROUND)
@@ -448,7 +424,7 @@ def tile_onedscaleparallelmha_pb_kernel(tc, q_rot, k_rot, v, feat_mask, wo_w, wo
             turn_w(half // 2, half % 2)
 
         def group_half(half):
-            group_w(half // 2, half % 2)
+            group_w(half // 2, half % 2, nc.vector.tensor_copy if half in (7, 10, 13) else nc.scalar.copy)
 
         def quantise_done(n, k):
             done = [half // 2 for half in halves_of(n) if half % 2 == 1]
@@ -458,10 +434,9 @@ def tile_onedscaleparallelmha_pb_kernel(tc, q_rot, k_rot, v, feat_mask, wo_w, wo
         for n in range(-QK_LEAD - 1, len(steps)):
             halves = halves_of(n)
             turn_e(n - 1, 1)
-            clear_e(n)
+            quantise_e(n - 2)
             maxima(n, 2)
             invert_rowsums(n - 2)
-            quantise_e(n - 2)
             quantise_ctx(n - 3)
             quantise_done(n - 1, 0)
             quantise_done(n - 1, 1)
@@ -469,18 +444,16 @@ def tile_onedscaleparallelmha_pb_kernel(tc, q_rot, k_rot, v, feat_mask, wo_w, wo
             first_product(n - 2)
             project(*chunk_of(n, 1), ALL)
             scores(n + 1, 0)
-            keep_q_and_k(n + 2, 0)
+            keep_q_and_k(n + 2)
             group_e(n - 1, 1)
             exponentials(n, 2)
             spread_over_partitions(n)
-            turn_q_and_k(n + 2, 1)
             turn_half(halves[0])
             scores(n + 1, 1)
             normalise(n - 2)
             maxima(n, 3)
             scale_and_store(*chunk_of(n, 0), nc.gpsimd)
             group_v(n)
-            keep_q_and_k(n + 2, 1)
             group_half(halves[0])
             exponentials(n, 3)
             turn_half(halves[1])
@@ -499,16 +472,16 @@ def tile_onedscaleparallelmha_pb_kernel(tc, q_rot, k_rot, v, feat_mask, wo_w, wo
             scores(n + 1, 3)
             maxima(n + 1, 1)
             group_e(n, 0)
-            turn_q_and_k(n + 3, 0)
+            turn_q_and_k(n + 3)
             group_half(halves[2])
             exponentials(n + 1, 1)
 
         n = len(steps)
-        before, last = BLOCK_ORDER[-2:]
+        before, last = BLOCKS - 2, BLOCKS - 1
         turn_e(n - 1, 1)
+        quantise_e(n - 2)
         invert_rowsums(n - 2)
         invert_rowsums(n - 1)
-        quantise_e(n - 2)
         quantise_ctx(n - 3)
         add_bias(before, 0)
         group_e(n - 1, 1)
@@ -518,7 +491,7 @@ def tile_onedscaleparallelmha_pb_kernel(tc, q_rot, k_rot, v, feat_mask, wo_w, wo
         turn_ctx(n - 2)
         quantise_e(n - 1)
         first_product(n - 1)
-        scale_and_store(before, 0, nc.vector)
+        scale_and_store(before, 0, nc.gpsimd)
         add_bias(before, 1)
         group_ctx(n - 2)
         project(before, 2, ALL)
@@ -526,12 +499,12 @@ def tile_onedscaleparallelmha_pb_kernel(tc, q_rot, k_rot, v, feat_mask, wo_w, wo
         turn_ctx(n - 1)
         quantise_ctx(n - 2)
         add_bias(before, 2)
-        scale_and_store(before, 1, nc.vector)
+        scale_and_store(before, 1, nc.gpsimd)
         group_ctx(n - 1)
         project(last, 0, range(2))
         project(last, 1, range(2))
         quantise_ctx(n - 1)
-        scale_and_store(before, 2, nc.vector)
+        scale_and_store(before, 2, nc.gpsimd)
         project(last, 0, [2])
         add_bias(last, 0)
         project(last, 1, [2])

@@ -35,6 +35,7 @@ W_PIECES = GROUPS * CHUNKS
 W_HALVES_PER_ROUND = 3
 W_FIRST_ROUND = 2
 KEPT_BY_VECTOR = range(2)
+TURNED_BY_PRODUCT = range(2, 9)
 QK_LEAD = 2
 
 
@@ -174,7 +175,12 @@ def tile_onedscaleparallelmha_pb_kernel(tc, q_rot, k_rot, v, feat_mask, wo_w, wo
             for side, rows in enumerate((q_sb, k_sb)):
                 for j in range(GROUP):
                     h = g * GROUP + j
-                    nc.tensor.transpose(qk_banks[n][:, side, j, :], rows[:, i, h * DH : (h + 1) * DH], ident_bf[:])
+                    turned = qk_banks[n][:, side, j, :]
+                    block = rows[:, i, h * DH : (h + 1) * DH]
+                    if n in TURNED_BY_PRODUCT:
+                        nc.tensor.matmul(out=turned, lhsT=block, rhs=ident_bf[:], start=True, stop=True)
+                    else:
+                        nc.tensor.transpose(turned, block, ident_bf[:])
 
         def keep_q_and_k(n):
             if not valid(n):

@@ -80,10 +80,10 @@ def tile_onedscaleparallelmha_pb_kernel(tc, q_rot, k_rot, v, feat_mask, wo_w, wo
             nc.sync.dma_start(out=q_sb[:, 0, cols], in_=q_rows[0][:, cols])
             nc.sync.dma_start(out=k_sb[:, 0, cols], in_=k_rows[0][:, cols])
         nc.sync.dma_start(out=fm_row[0:1, :], in_=feat_mask.unsqueeze(0))
-        nc.sync.dma_start(
-            out=v_sb[:].rearrange("p (c e) f -> p c (e f)", c=2),
-            in_=v.rearrange("b (c p e) h d -> p (b c) (e h d)", c=2, e=2),
-        )
+        v_rows = v.rearrange("b (c p e) h d -> (b c) p e (h d)", c=2, e=2)
+        for cols in (slice(0, GROUP * DH), slice(GROUP * DH, E)):
+            for c in range(2):
+                nc.sync.dma_start(out=v_sb[:, 2 * c : 2 * c + 2, cols], in_=v_rows[c][:, :, cols])
         load(q_rows, q_sb, 1)
         load(k_rows, k_sb, 1)
         load_w(0)
@@ -306,17 +306,20 @@ def tile_onedscaleparallelmha_pb_kernel(tc, q_rot, k_rot, v, feat_mask, wo_w, wo
                 in_=e_banks[n, pair][:].rearrange("p c j t -> p (j t) c"),
             )
 
-        def quantise_e(n):
+        def quantise_e(n, first=0, count=GROUP):
             if not valid(n):
                 return
-            e_codes = work.tile([P, GROUP * P], U32, align_bytes=64)
-            e_scales = work.tile([P, GROUP * P], U8, align_bytes=64)
+            if first == 0:
+                e_codes = work.tile([P, GROUP * P], U32, name="e_codes", align_bytes=64)
+                e_scales = work.tile([P, GROUP * P], U8, name="e_scales", align_bytes=64)
+                e_quantised[n] = (e_codes, e_scales)
+            e_codes, e_scales = e_quantised[n]
+            cols = slice(first * P, (first + count) * P)
             nc.vector.quantize_mx(
-                out=e_codes[:].bitcast(FP8X4),
-                scales=e_scales[:],
-                in_=e_grouped[n][:].rearrange("p j t a -> p (j t a)"),
+                out=e_codes[:, cols].bitcast(FP8X4),
+                scales=e_scales[:, cols],
+                in_=e_grouped[n][:, first : first + count].rearrange("p j t a -> p (j t a)"),
             )
-            e_quantised[n] = (e_codes, e_scales)
 
         def invert_rowsums(n):
             if not valid(n):
@@ -324,12 +327,13 @@ def tile_onedscaleparallelmha_pb_kernel(tc, q_rot, k_rot, v, feat_mask, wo_w, wo
             inverses[n] = small.tile([P, GROUP], F32, name="inverse")
             nc.vector.reciprocal(out=inverses[n][:], in_=rowsums[n][:])
 
-        def first_product(n):
+        def first_product(n, first=0, count=GROUP):
             if not valid(n):
                 return
-            c_banks[n] = ps_ctx.tile([P, GROUP, P], F32, name="c_ps")
+            if first == 0:
+                c_banks[n] = ps_ctx.tile([P, GROUP, P], F32, name="c_ps")
             e_codes, e_scales = e_quantised[n]
-            for j in range(GROUP):
+            for j in range(first, first + count):
                 h = steps[n][1] * GROUP + j
                 nc.tensor.matmul_mx(
                     out=c_banks[n][:, j, :],
@@ -341,11 +345,12 @@ def tile_onedscaleparallelmha_pb_kernel(tc, q_rot, k_rot, v, feat_mask, wo_w, wo
                     stop=True,
                 )
 
-        def normalise(n):
+        def normalise(n, first=0, count=GROUP):
             if not valid(n):
                 return
-            contexts[n] = work.tile([P, GROUP * DH], BF16, name="ctx_sb")
-            for j in range(GROUP):
+            if first == 0:
+                contexts[n] = work.tile([P, GROUP * DH], BF16, name="ctx_sb")
+            for j in range(first, first + count):
                 h = steps[n][1] * GROUP + j
                 nc.vector.scalar_tensor_tensor(
                     out=contexts[n][:, j * DH : (j + 1) * DH],
@@ -356,11 +361,12 @@ def tile_onedscaleparallelmha_pb_kernel(tc, q_rot, k_rot, v, feat_mask, wo_w, wo
                     op1=ALU.mult,
                 )
 
-        def turn_ctx(n):
+        def turn_ctx(n, halves=range(2)):
             if not valid(n):
                 return
-            ctx_banks[n] = ps_turn.tile([P, 2, P], F32, name="ctx_bank", tag="turn")
-            for c in range(2):
+            if halves[0] == 0:
+                ctx_banks[n] = ps_turn.tile([P, 2, P], F32, name="ctx_bank", tag="turn")
+            for c in halves:
                 nc.tensor.transpose(
                     ctx_banks[n][:, c, :], contexts[n][:].bitcast(F32)[:, c * P : (c + 1) * P], ident_f32[:]
                 )
@@ -430,7 +436,7 @@ def tile_onedscaleparallelmha_pb_kernel(tc, q_rot, k_rot, v, feat_mask, wo_w, wo
             turn_w(half // 2, half % 2)
 
         def group_half(half):
-            group_w(half // 2, half % 2, nc.vector.tensor_copy if half in (7, 10, 13) else nc.scalar.copy)
+            group_w(half // 2, half % 2, nc.vector.tensor_copy if half in (7, 13) else nc.scalar.copy)
 
         def quantise_done(n, k):
             done = [half // 2 for half in halves_of(n) if half % 2 == 1]
@@ -487,29 +493,31 @@ def tile_onedscaleparallelmha_pb_kernel(tc, q_rot, k_rot, v, feat_mask, wo_w, wo
         turn_e(n - 1, 1)
         quantise_e(n - 2)
         invert_rowsums(n - 2)
-        invert_rowsums(n - 1)
         quantise_ctx(n - 3)
         add_bias(before, 0)
+        invert_rowsums(n - 1)
         group_e(n - 1, 1)
         first_product(n - 2)
         project(before, 1, ALL)
         normalise(n - 2)
         turn_ctx(n - 2)
-        quantise_e(n - 1)
-        first_product(n - 1)
+        for first in (0, 2):
+            quantise_e(n - 1, first, 2)
+            first_product(n - 1, first, 2)
         scale_and_store(before, 0, nc.gpsimd)
         add_bias(before, 1)
         group_ctx(n - 2)
         project(before, 2, ALL)
-        normalise(n - 1)
-        turn_ctx(n - 1)
+        for half in range(2):
+            normalise(n - 1, 2 * half, 2)
+            turn_ctx(n - 1, [half])
         quantise_ctx(n - 2)
-        add_bias(before, 2)
-        scale_and_store(before, 1, nc.gpsimd)
         group_ctx(n - 1)
         project(last, 0, range(2))
         project(last, 1, range(2))
         quantise_ctx(n - 1)
+        add_bias(before, 2)
+        scale_and_store(before, 1, nc.gpsimd)
         scale_and_store(before, 2, nc.gpsimd)
         project(last, 0, [2])
         add_bias(last, 0)

import math
from contextlib import ExitStack

import concourse.mybir as mybir
from concourse.masks import make_identity

BF16 = mybir.dt.bfloat16
F32 = mybir.dt.float32
U32 = mybir.dt.uint32
I32 = mybir.dt.int32
U8 = mybir.dt.uint8
FP8X4 = mybir.dt.float8_e4m3fn_x4
ALU = mybir.AluOpType
ACT = mybir.ActivationFunctionType
AXIS = mybir.AxisListType

P = 128
PACK = 4
S = 512
H = 12
DH = 128
E = H * DH
BLOCKS = S // P
GROUP = PACK
GROUPS = H // GROUP
CHUNK = 512
CHUNKS = E // CHUNK
SCALE = 1.0 / math.sqrt(DH)
MASK_RAW = -10000.0 * math.sqrt(DH)

FLOPS = 2 * H * S * S * DH * 2 + 2 * S * E * E


W_PIECES = GROUPS * CHUNKS
W_HALVES_PER_ROUND = 3
W_FIRST_ROUND = 2
KEPT_BY_VECTOR = range(2)
TURNED_BY_PRODUCT = range(2, 9)
QK_LEAD = 2


def tile_onedscaleparallelmha_pb_kernel(tc, q_rot, k_rot, v, feat_mask, wo_w, wo_b, out):
    nc = tc.nc
    steps = [(i, g) for i in range(BLOCKS) for g in range(GROUPS)]

    def valid(n):
        return 0 <= n < len(steps)

    with ExitStack() as stack:
        const = stack.enter_context(tc.tile_pool(name="const", bufs=1))
        keep = stack.enter_context(tc.tile_pool(name="keep", bufs=1))
        work = stack.enter_context(tc.tile_pool(name="work", bufs=3))
        small = stack.enter_context(tc.tile_pool(name="small", bufs=12))
        ps_scores = stack.enter_context(tc.psum_pool(name="ps_scores", bufs=4))
        ps_turn = stack.enter_context(tc.psum_pool(name="ps_turn", bufs=3))
        ps_ctx = stack.enter_context(tc.psum_pool(name="ps_ctx", bufs=1))
        stack.enter_context(tc.manual_schedule())

        q_rows = q_rot.rearrange("b (i p) h d -> (b i) p (h d)", p=P)
        k_rows = k_rot.rearrange("b (i p) h d -> (b i) p (h d)", p=P)
        w_rows = wo_w.rearrange("(b p) f -> p b f", p=P)
        q_sb = keep.tile([P, BLOCKS, E], BF16)
        k_sb = keep.tile([P, BLOCKS, E], BF16)
        v_sb = keep.tile([P, PACK, E], BF16)
        w_sb = keep.tile([P, H, E], BF16)
        fm_row = const.tile([P, E], BF16)
        nc.vector.memset(fm_row[:].bitcast(I32), 0)
        fm_bc = const.tile([P, E], BF16)
        b_bc = const.tile([P, E], BF16)

        def load(rows, sb, i):
            nc.sync.dma_start(out=sb[:, i, :], in_=rows[i])

        ALL = range(GROUPS)

        def load_w(c):
            nc.sync.dma_start(out=w_sb[:, 4 * c : 4 * c + 4, :], in_=w_rows[:, 4 * c : 4 * c + 4, :])

        for cols in (slice(0, GROUP * DH), slice(GROUP * DH, E)):
            nc.sync.dma_start(out=q_sb[:, 0, cols], in_=q_rows[0][:, cols])
            nc.sync.dma_start(out=k_sb[:, 0, cols], in_=k_rows[0][:, cols])
        nc.sync.dma_start(out=fm_row[0:1, :], in_=feat_mask.unsqueeze(0))
        v_rows = v.rearrange("b (c p e) h d -> (b c) p e (h d)", c=2, e=2)
        for cols in (slice(0, GROUP * DH), slice(GROUP * DH, E)):
            for c in range(2):
                nc.sync.dma_start(out=v_sb[:, 2 * c : 2 * c + 2, cols], in_=v_rows[c][:, :, cols])
        load(q_rows, q_sb, 1)
        load(k_rows, k_sb, 1)
        load_w(0)
        load(q_rows, q_sb, 2)
        load(k_rows, k_sb, 2)
        load_w(1)
        load_w(2)
        load(q_rows, q_sb, 3)
        load(k_rows, k_sb, 3)
        nc.sync.dma_start(out=b_bc[:], in_=wo_b.partition_broadcast(P))

        e_sb = keep.tile([P, 2 * GROUP, S], BF16)
        nc.vector.memset(e_sb[:].rearrange("p r u -> p (r u)").bitcast(I32), 0)
        ident_bf = const.tile([P, P], BF16)
        make_identity(nc, ident_bf[:])
        ident_f32 = const.tile([P, P], F32)
        make_identity(nc, ident_f32[:])
        mask_f32 = const.tile([P, P], F32)
        nc.gpsimd.memset(mask_f32[:], 0.0)
        nc.gpsimd.affine_select(
            out=mask_f32[:],
            in_=mask_f32[:],
            compare_op=ALU.is_ge,
            fill=MASK_RAW,
            base=0,
            pattern=[[-1, P]],
            channel_multiplier=1,
        )
        mask_bf = const.tile([P, P], BF16)
        nc.vector.tensor_copy(out=mask_bf[:], in_=mask_f32[:])
        ones_bf = const.tile([P, P], BF16)
        nc.vector.memset(ones_bf[:], 1.0)

        qk_t = keep.tile([P, 2, H, S], BF16)
        q_t = qk_t[:, 0]
        k_t = qk_t[:, 1]
        v_codes = keep.tile([P, E], U32, align_bytes=64)
        v_scales = keep.tile([P, E], U8, align_bytes=64)
        w_codes = keep.tile([P, GROUPS, E], U32, align_bytes=64)
        w_scales = keep.tile([P, GROUPS, E], U8, align_bytes=64)
        ctx_codes = keep.tile([P, GROUPS, S], U32, align_bytes=64)
        ctx_scales = keep.tile([P, GROUPS, S], U8, align_bytes=64)
        out_rows = out.rearrange("b (i p) o -> (b i) p o", p=P)

        qk_banks = {}
        score_banks = {}
        scaled_scores = {}
        shifts = {}
        rowsums = {}
        e_banks = {}
        e_grouped = {}
        e_quantised = {}
        c_banks = {}
        inverses = {}
        contexts = {}
        ctx_banks = {}
        ctx_grouped = {}
        v_grouped = {}
        w_banks = {}
        w_grouped = {}
        out_banks = {}
        biased = {}

        def e_row(n, j):
            return (n % 2) * GROUP + j


        def spread_over_partitions(k):
            first = 2 * k * CHUNK
            width = min(2 * CHUNK, E - first)
            if k < 0 or width <= 0:
                return
            repeated = ps_scores.tile([P, width], BF16, name="repeated", tag="bank")
            for at in range(0, width, CHUNK):
                nc.tensor.matmul(
                    out=repeated[:, at : at + CHUNK],
                    lhsT=ones_bf[:],
                    rhs=fm_row[:, first + at : first + at + CHUNK],
                    start=True,
                    stop=True,
                )
            nc.scalar.copy(out=fm_bc[:, first : first + width], in_=repeated[:])

        def turn_q_and_k(n):
            if not valid(n):
                return
            i, g = steps[n]
            qk_banks[n] = ps_turn.tile([P, 2, GROUP, P], BF16, name="qk_bank", tag="turn")
            for side, rows in enumerate((q_sb, k_sb)):
                for j in range(GROUP):
                    h = g * GROUP + j
                    turned = qk_banks[n][:, side, j, :]
                    block = rows[:, i, h * DH : (h + 1) * DH]
                    if n in TURNED_BY_PRODUCT:
                        nc.tensor.matmul(out=turned, lhsT=block, rhs=ident_bf[:], start=True, stop=True)
                    else:
                        nc.tensor.transpose(turned, block, ident_bf[:])

        def keep_q_and_k(n):
            if not valid(n):
                return
            i, g = steps[n]
            move = nc.vector.tensor_copy if n in KEPT_BY_VECTOR else nc.scalar.copy
            move(out=qk_t[:, :, g * GROUP : (g + 1) * GROUP, i * P : (i + 1) * P], in_=qk_banks[n][:])

        def group_v(g):
            if not 0 <= g < GROUPS:
                return
            cols = slice(g * CHUNK, (g + 1) * CHUNK)
            rows = v_sb[:, :, cols].rearrange("p a f -> p f a")
            v_grouped[g] = work.tile([P, CHUNK, PACK], BF16, name="v_grouped", tag="v_grouped", bufs=2, align_bytes=64)
            nc.vector.tensor_copy(out=v_grouped[g][:], in_=rows)

        def quantise_v(g):
            if not 0 <= g < GROUPS:
                return
            cols = slice(g * CHUNK, (g + 1) * CHUNK)
            nc.vector.quantize_mx(
                out=v_codes[:, cols].bitcast(FP8X4),
                scales=v_scales[:, cols],
                in_=v_grouped[g][:].rearrange("p f a -> p (f a)"),
            )

        def turn_w(piece, half):
            if not 0 <= piece < W_PIECES:
                return
            c, g = piece // GROUPS, piece % GROUPS
            w_banks[piece, half] = ps_turn.tile([P, 2, 2, P], F32, name="w_bank", tag="turn")
            for u in range(2):
                for b in range(2):
                    w_words = w_sb[:, 4 * c + 2 * half + b, :].bitcast(F32)
                    first = 256 * g + 128 * u
                    nc.tensor.transpose(w_banks[piece, half][:, u, b, :], w_words[:, first : first + P], ident_f32[:])

        def group_w(piece, half, move):
            if not 0 <= piece < W_PIECES:
                return
            if half == 0:
                w_grouped[piece] = work.tile([P, CHUNK, PACK], BF16, name="w_grouped", tag="grouped", align_bytes=64)
            words = w_grouped[piece][:].rearrange("p o j -> p (o j)").bitcast(F32).rearrange("p (o u) -> p o u", u=2)
            move(
                out=words[:, half * 2 * P : (half + 1) * 2 * P, :],
                in_=w_banks[piece, half][:].rearrange("p u b o -> p (b o) u"),
            )

        def quantise_w(piece):
            if not 0 <= piece < W_PIECES:
                return
            c, g = piece // GROUPS, piece % GROUPS
            cols = slice(c * CHUNK, (c + 1) * CHUNK)
            nc.vector.quantize_mx(
                out=w_codes[:, g, cols].bitcast(FP8X4),
                scales=w_scales[:, g, cols],
                in_=w_grouped[piece][:].rearrange("p o j -> p (o j)"),
            )

        def scores(n, j):
            if not valid(n):
                return
            i, g = steps[n]
            h = g * GROUP + j
            keys = (i + 1) * P
            s_ps = ps_scores.tile([P, S], F32, name="score_bank", tag="bank")
            score_banks[n, j] = s_ps
            nc.tensor.matmul(
                out=s_ps[:, :keys], lhsT=q_t[:, h, i * P : (i + 1) * P], rhs=k_t[:, h, :keys], start=True, stop=False
            )
            nc.tensor.matmul(out=s_ps[:, i * P : keys], lhsT=ident_bf[:], rhs=mask_bf[:], start=False, stop=True)

        def maxima(n, j):
            if not valid(n):
                return
            keys = (steps[n][0] + 1) * P
            s_ps = score_banks[n, j]
            scaled_scores[n, j] = work.tile([P, S], F32, name="scaled", bufs=2 * GROUP)
            shifts[n, j] = small.tile([P, 1], F32, name="shift")
            nc.vector.tensor_scalar(
                out=scaled_scores[n, j][:, :keys],
                in0=s_ps[:, :keys],
                scalar1=-SCALE,
                scalar2=None,
                op0=ALU.mult,
                op1=ALU.min,
                accum_out=shifts[n, j][:],
            )

        def exponentials(n, j):
            if not valid(n):
                return
            keys = (steps[n][0] + 1) * P
            if j == 0:
                rowsums[n] = small.tile([P, GROUP], F32, name="rowsum")
            nc.scalar.activation(
                out=e_sb[:, e_row(n, j), :keys],
                in_=scaled_scores[n, j][:, :keys],
                func=ACT.Exp,
                bias=shifts[n, j][:],
                scale=-1.0,
                accum_out=rowsums[n][:, j : j + 1],
            )

        def turn_e(n, pair):
            if not valid(n):
                return
            e_banks[n, pair] = ps_turn.tile([P, 2, 2, P], F32, name="e_bank", tag="turn")
            for c in range(2):
                for j in range(2):
                    words = e_sb[:, e_row(n, 2 * pair + j), :].bitcast(F32)
                    nc.tensor.transpose(e_banks[n, pair][:, c, j, :], words[:, c * P : (c + 1) * P], ident_f32[:])

        def group_e(n, pair):
            if not valid(n):
                return
            if pair == 0:
                e_grouped[n] = work.tile([P, GROUP, P, PACK], BF16, name="e_grouped", bufs=2, align_bytes=64)
            words = e_grouped[n][:].rearrange("p j t a -> p (j t a)").bitcast(F32)
            words = words.rearrange("p (r c) -> p r c", c=2)
            nc.scalar.copy(
                out=words[:, pair * 2 * P : (pair + 1) * 2 * P, :],
                in_=e_banks[n, pair][:].rearrange("p c j t -> p (j t) c"),
            )

        def quantise_e(n, first=0, count=GROUP):
            if not valid(n):
                return
            if first == 0:
                e_codes = work.tile([P, GROUP * P], U32, name="e_codes", align_bytes=64)
                e_scales = work.tile([P, GROUP * P], U8, name="e_scales", align_bytes=64)
                e_quantised[n] = (e_codes, e_scales)
            e_codes, e_scales = e_quantised[n]
            cols = slice(first * P, (first + count) * P)
            nc.vector.quantize_mx(
                out=e_codes[:, cols].bitcast(FP8X4),
                scales=e_scales[:, cols],
                in_=e_grouped[n][:, first : first + count].rearrange("p j t a -> p (j t a)"),
            )

        def invert_rowsums(n):
            if not valid(n):
                return
            inverses[n] = small.tile([P, GROUP], F32, name="inverse")
            nc.vector.reciprocal(out=inverses[n][:], in_=rowsums[n][:])

        def first_product(n, first=0, count=GROUP):
            if not valid(n):
                return
            if first == 0:
                c_banks[n] = ps_ctx.tile([P, GROUP, P], F32, name="c_ps")
            e_codes, e_scales = e_quantised[n]
            for j in range(first, first + count):
                h = steps[n][1] * GROUP + j
                nc.tensor.matmul_mx(
                    out=c_banks[n][:, j, :],
                    lhsT=e_codes[:, j * P : (j + 1) * P].bitcast(FP8X4),
                    lhsT_scale=e_scales[:, j * P : (j + 1) * P],
                    rhs=v_codes[:, h * DH : (h + 1) * DH].bitcast(FP8X4),
                    rhs_scale=v_scales[:, h * DH : (h + 1) * DH],
                    start=True,
                    stop=True,
                )

        def normalise(n, first=0, count=GROUP):
            if not valid(n):
                return
            if first == 0:
                contexts[n] = work.tile([P, GROUP * DH], BF16, name="ctx_sb")
            for j in range(first, first + count):
                h = steps[n][1] * GROUP + j
                nc.vector.scalar_tensor_tensor(
                    out=contexts[n][:, j * DH : (j + 1) * DH],
                    in0=c_banks[n][:, j, :],
                    scalar=inverses[n][:, j : j + 1],
                    in1=fm_bc[:, h * DH : (h + 1) * DH],
                    op0=ALU.mult,
                    op1=ALU.mult,
                )

        def turn_ctx(n, halves=range(2)):
            if not valid(n):
                return
            if halves[0] == 0:
                ctx_banks[n] = ps_turn.tile([P, 2, P], F32, name="ctx_bank", tag="turn")
            for c in halves:
                nc.tensor.transpose(
                    ctx_banks[n][:, c, :], contexts[n][:].bitcast(F32)[:, c * P : (c + 1) * P], ident_f32[:]
                )

        def group_ctx(n):
            if not valid(n):
                return
            ctx_grouped[n] = work.tile([P, P, PACK], BF16, name="ctx_grouped", align_bytes=64)
            nc.scalar.copy(
                out=ctx_grouped[n][:].rearrange("p t a -> p (t a)").bitcast(F32).rearrange("p (t c) -> p t c", c=2),
                in_=ctx_banks[n][:].rearrange("p c t -> p t c"),
            )

        def quantise_ctx(n):
            if not valid(n):
                return
            i, g = steps[n]
            nc.vector.quantize_mx(
                out=ctx_codes[:, g, i * P : (i + 1) * P].bitcast(FP8X4),
                scales=ctx_scales[:, g, i * P : (i + 1) * P],
                in_=ctx_grouped[n][:].rearrange("p t a -> p (t a)"),
            )

        def project(i, c, groups):
            if not 0 <= i < BLOCKS:
                return
            if groups[0] == 0:
                out_banks[i, c] = ps_scores.tile([P, CHUNK], F32, name="out_bank", tag="bank")
            cols = slice(c * CHUNK, (c + 1) * CHUNK)
            for g in groups:
                nc.tensor.matmul_mx(
                    out=out_banks[i, c][:],
                    lhsT=ctx_codes[:, g, i * P : (i + 1) * P].bitcast(FP8X4),
                    lhsT_scale=ctx_scales[:, g, i * P : (i + 1) * P],
                    rhs=w_codes[:, g, cols].bitcast(FP8X4),
                    rhs_scale=w_scales[:, g, cols],
                    start=(g == 0),
                    stop=(g == GROUPS - 1),
                )

        def add_bias(i, c):
            if not 0 <= i < BLOCKS:
                return
            biased[i, c] = work.tile([P, CHUNK], F32, name="biased", bufs=4)
            nc.vector.tensor_tensor(
                out=biased[i, c][:], in0=out_banks[i, c][:], in1=b_bc[:, c * CHUNK : (c + 1) * CHUNK], op=ALU.add
            )

        def scale_and_store(i, c, engine):
            if not 0 <= i < BLOCKS:
                return
            cols = slice(c * CHUNK, (c + 1) * CHUNK)
            result = work.tile([P, CHUNK], F32, name="result", bufs=6)
            engine.tensor_tensor(out=result[:], in0=biased[i, c][:], in1=fm_bc[:, cols], op=ALU.mult)
            nc.sync.dma_start(out=out_rows[i][:, cols], in_=result[:])

        finished = {6: [(0, 0)], 7: [(0, 1)], 9: [(0, 2), (1, 0)], 10: [(1, 1)], 11: [(1, 2)], 12: [(2, 0)]}

        def chunk_of(n, k):
            found = finished.get(n, [])
            return found[k] if k < len(found) else (-1, 0)

        def halves_of(n):
            return range((n - W_FIRST_ROUND) * W_HALVES_PER_ROUND, (n - W_FIRST_ROUND + 1) * W_HALVES_PER_ROUND)

        def turn_half(half):
            turn_w(half // 2, half % 2)

        def group_half(half):
            group_w(half // 2, half % 2, nc.vector.tensor_copy if half in (7, 13) else nc.scalar.copy)

        def quantise_done(n, k):
            done = [half // 2 for half in halves_of(n) if half % 2 == 1]
            if k < len(done):
                quantise_w(done[k])

        for n in range(-QK_LEAD - 1, len(steps)):
            halves = halves_of(n)
            turn_e(n - 1, 1)
            quantise_e(n - 2)
            maxima(n, 2)
            invert_rowsums(n - 2)
            quantise_ctx(n - 3)
            quantise_done(n - 1, 0)
            quantise_done(n - 1, 1)
            add_bias(*chunk_of(n, 0))
            first_product(n - 2)
            project(*chunk_of(n, 1), ALL)
            scores(n + 1, 0)
            keep_q_and_k(n + 2)
            group_e(n - 1, 1)
            exponentials(n, 2)
            spread_over_partitions(n)
            turn_half(halves[0])
            scores(n + 1, 1)
            normalise(n - 2)
            maxima(n, 3)
            scale_and_store(*chunk_of(n, 0), nc.gpsimd)
            group_v(n)
            group_half(halves[0])
            exponentials(n, 3)
            turn_half(halves[1])
            turn_ctx(n - 2)
            scores(n + 1, 2)
            add_bias(*chunk_of(n, 1))
            scale_and_store(*chunk_of(n, 1), nc.gpsimd)
            maxima(n + 1, 0)
            quantise_v(n - 1)
            group_half(halves[1])
            group_ctx(n - 2)
            exponentials(n + 1, 0)
            turn_e(n, 0)
            project(*chunk_of(n + 1, 0), ALL)
            turn_half(halves[2])
            scores(n + 1, 3)
            maxima(n + 1, 1)
            group_e(n, 0)
            turn_q_and_k(n + 3)
            group_half(halves[2])
            exponentials(n + 1, 1)

        n = len(steps)
        before, last = BLOCKS - 2, BLOCKS - 1
        turn_e(n - 1, 1)
        quantise_e(n - 2)
        invert_rowsums(n - 2)
        quantise_ctx(n - 3)
        add_bias(before, 0)
        invert_rowsums(n - 1)
        group_e(n - 1, 1)
        first_product(n - 2)
        project(before, 1, ALL)
        normalise(n - 2)
        turn_ctx(n - 2)
        for first in (0, 2):
            quantise_e(n - 1, first, 2)
            first_product(n - 1, first, 2)
        scale_and_store(before, 0, nc.gpsimd)
        add_bias(before, 1)
        group_ctx(n - 2)
        project(before, 2, ALL)
        for half in range(2):
            normalise(n - 1, 2 * half, 2)
            turn_ctx(n - 1, [half])
        quantise_ctx(n - 2)
        group_ctx(n - 1)
        project(last, 0, range(2))
        project(last, 1, range(2))
        quantise_ctx(n - 1)
        add_bias(before, 2)
        scale_and_store(before, 1, nc.gpsimd)
        scale_and_store(before, 2, nc.gpsimd)
        project(last, 0, [2])
        add_bias(last, 0)
        project(last, 1, [2])
        add_bias(last, 1)
        project(last, 2, range(2))
        scale_and_store(last, 0, nc.vector)
        project(last, 2, [2])
        add_bias(last, 2)
        scale_and_store(last, 1, nc.vector)
        scale_and_store(last, 2, nc.vector)
